import numpy as np
import ml_dtypes


def mxq(x, axis, fmt="e4m3"):
    dtype, down = {"e4m3": (ml_dtypes.float8_e4m3fn, 7), "e5m2": (ml_dtypes.float8_e5m2, 14)}[fmt]
    v = np.moveaxis(np.asarray(x, np.float32).astype(ml_dtypes.bfloat16).astype(np.float64), axis, -1)
    blocks = v.reshape(v.shape[:-1] + (-1, 32))
    amax = np.abs(blocks).max(-1, keepdims=True)
    byte = np.maximum(np.where(amax > 0, np.frexp(amax)[1] - 1 + 127, 0) - down, 1)
    scale = np.exp2(byte - 127.0)
    codes = (blocks / scale).astype(np.float32).astype(dtype).astype(np.float64)
    return np.moveaxis((codes * scale).reshape(v.shape), -1, axis)


WIDE = False


def mx_kscale(k):
    if not WIDE:
        return np.ones(k)
    levels = np.array([10, -10, 5, -5, 0])
    a = np.random.permutation(np.resize(levels, k // 512 * 4)).reshape(k // 512, 4)
    idx = np.arange(k)
    return np.exp2(a[idx // 512, idx % 128 // 32])


BF16 = ml_dtypes.bfloat16


def bf(x):
    return np.asarray(x, np.float32).astype(BF16)


def f64(x):
    return np.asarray(x).astype(np.float64)


B, N, D, H = 4, 32, 512, 128
D2 = D + D
D3 = D2 + D
ERF_TERMS = 100
ERF_CLIP = 6.0


def erf(z):
    z = np.minimum(np.maximum(z, -ERF_CLIP), ERF_CLIP)
    zz = 2.0 * z * z
    term = z
    tot = z
    for n in range(1, ERF_TERMS):
        term = term * zz / (2 * n + 1)
        tot = tot + term
    return 2.0 / np.sqrt(np.pi) * np.exp(-z * z) * tot


def gelu(v):
    return 0.5 * v * (1.0 + erf(v / np.sqrt(2.0)))


def setup_inputs():
    s = mx_kscale(D)
    r = np.concatenate([s, s, np.ones(D)])
    return {
        "h": bf(np.random.standard_normal((B, N, D)) * s),
        "edge_features": bf(np.random.standard_normal((B, N, N, D))),
        "Wu1_w": bf(np.random.standard_normal((D3, D)) / np.sqrt(D3) / r[:, None]),
        "Wu1_b": bf(np.random.standard_normal(D) * 0.2),
        "Wu2_w": bf(np.random.standard_normal((D, D)) * 1.5 / np.sqrt(D)),
        "Wu2_b": bf(np.random.standard_normal(D) * 0.2),
    }


def reference(h, edge_features, Wu1_w, Wu1_b, Wu2_w, Wu2_b):
    ef = f64(edge_features)
    hq = mxq(f64(h), 2, "e4m3")
    w1 = mxq(f64(Wu1_w), 0, "e4m3")
    p_i = hq @ w1[:D]
    p_j = hq @ w1[D:D2]
    p_e = mxq(ef, 3, "e4m3") @ w1[D2:]
    pre = p_i[:, :, None, :] + p_j[:, None, :, :] + p_e + f64(Wu1_b)
    u = gelu(pre)
    return ef + ((mxq(u, 3, "e4m3") @ mxq(f64(Wu2_w), 0, "e4m3")) + f64(Wu2_b))

@@ -1,0 +1,272 @@
+from contextlib import ExitStack
+
+import concourse.masks as masks
+import concourse.mybir as mybir
+
+F32 = mybir.dt.float32
+BF16 = mybir.dt.bfloat16
+I32 = mybir.dt.int32
+U32 = mybir.dt.uint32
+U8 = mybir.dt.uint8
+FP8X4 = mybir.dt.float8_e4m3fn_x4
+ADD = mybir.AluOpType.add
+GELU = mybir.ActivationFunctionType.Gelu
+
+P = 128
+PACK = 4
+D = P * PACK
+GRAPHS = 4
+NODES = 32
+EDGES = GRAPHS * NODES * NODES
+GROUP = 512
+GROUPS = EDGES // GROUP
+ROWS = GROUP // P
+I_OF_GROUP = GROUP // NODES
+WORD_BYTES = 4
+
+FLOPS = 2 * D * D * (2 * GRAPHS * NODES + 2 * EDGES)
+
+
+def tile_graphconvlayer_pb_kernel(tc, h, edge_features, Wu1_w, Wu1_b, Wu2_w, Wu2_b, out):
+    nc = tc.nc
+    h_rows = h.rearrange("b n d -> (b n) d")
+    ef_rows = edge_features.rearrange("b i j d -> (b i j) d")
+    out_rows = out.rearrange("b i j d -> (b i j) d")
+
+    with ExitStack() as ctx:
+        keep = ctx.enter_context(tc.tile_pool(name="keep", bufs=1))
+        stage = ctx.enter_context(tc.tile_pool(name="stage", bufs=2))
+        results = ctx.enter_context(tc.tile_pool(name="results", bufs=3))
+        flip_banks = ctx.enter_context(tc.psum_pool(name="flip_banks", bufs=2))
+        mx_banks = ctx.enter_context(tc.psum_pool(name="mx_banks", bufs=6))
+
+        h_sb = keep.tile([P, D], BF16)
+        nc.sync.dma_start(out=h_sb[:], in_=h_rows)
+        w_raw = []
+        for blk in range(3):
+            raw = keep.tile([P, PACK * D], BF16, name="w_raw%d" % blk)
+            nc.sync.dma_start(
+                out=raw[:].rearrange("p (u e c) -> p u e c", u=2, e=2),
+                in_=Wu1_w[blk * D : (blk + 1) * D, :].rearrange("(u p e) c -> p u e c", u=2, e=2),
+            )
+            w_raw.append(raw)
+        ef_sb = []
+        for g in range(GROUPS):
+            if g == 1:
+                raw = keep.tile([P, PACK * D], BF16, name="w_raw3")
+                nc.sync.dma_start(
+                    out=raw[:].rearrange("p (t c) -> p t c", t=PACK),
+                    in_=Wu2_w.rearrange("(t p) c -> p t c", p=P),
+                )
+                w_raw.append(raw)
+            ef_g = keep.tile([P, ROWS * D], BF16, name="ef%d" % g)
+            nc.sync.dma_start(
+                out=ef_g[:].rearrange("p (r d) -> p r d", r=ROWS),
+                in_=ef_rows[g * GROUP : (g + 1) * GROUP, :].rearrange("(r p) d -> p r d", p=P),
+            )
+            ef_sb.append(ef_g)
+
+        b1_rows = keep.tile([P, P], BF16)
+        nc.vector.memset(b1_rows[:], 0.0)
+        nc.scalar.dma_start(out=b1_rows[0:PACK, :], in_=Wu1_b.rearrange("(t p) -> t p", p=P))
+        b2_all = keep.tile([P, D], BF16)
+        nc.scalar.dma_start(out=b2_all[:], in_=Wu2_b.partition_broadcast(P))
+
+        warm = keep.tile([P, 1], F32)
+        nc.vector.memset(warm[:], 0.0)
+        nc.scalar.activation(out=warm[:], in_=warm[:], func=GELU)
+
+        ident = keep.tile([P, P], F32)
+        masks.make_identity(nc, ident[:])
+
+        h_flip = flip_banks.tile([P, 2, P], F32, tag="flip")
+        for u in range(2):
+            nc.tensor.transpose(h_flip[:, u, :], h_sb[:].bitcast(F32)[:, u * P : (u + 1) * P], ident[:])
+        h_flip_nu = h_flip[:].rearrange("p u n -> p n u")
+        h_once = keep.tile([P, GRAPHS * NODES * PACK], BF16, align_bytes=64)
+        nc.vector.tensor_copy(out=h_once[:].bitcast(F32).rearrange("p (n u) -> p n u", u=2), in_=h_flip_nu)
+        h_four = keep.tile([P, GRAPHS * NODES * WORD_BYTES * PACK], BF16, align_bytes=64)
+        nc.vector.tensor_copy(
+            out=h_four[:].bitcast(F32).rearrange("p (n w u) -> p n w u", w=WORD_BYTES, u=2),
+            in_=h_flip_nu.unsqueeze(2).to_broadcast([P, GRAPHS * NODES, WORD_BYTES, 2]),
+        )
+        once_codes = keep.tile([P, GRAPHS * NODES], U32, align_bytes=64)
+        once_scales = keep.tile([P, GRAPHS * NODES], U8, align_bytes=64)
+        four_codes = keep.tile([P, GRAPHS * NODES * WORD_BYTES], U32, align_bytes=64)
+        four_scales = keep.tile([P, GRAPHS * NODES * WORD_BYTES], U8, align_bytes=64)
+        nc.vector.memset(once_scales[:].bitcast(I32), 0)
+        nc.vector.memset(four_scales[:].bitcast(I32), 0)
+        nc.vector.quantize_mx(out=once_codes[:].bitcast(FP8X4), scales=once_scales[:], in_=h_once[:])
+        nc.vector.quantize_mx(out=four_codes[:].bitcast(FP8X4), scales=four_scales[:], in_=h_four[:])
+
+        hi_codes = keep.tile([P, EDGES], U32, align_bytes=64)
+        hi_scales = keep.tile([P, EDGES], U8, align_bytes=64)
+        hj_codes = keep.tile([P, GRAPHS * GROUP], U32, align_bytes=64)
+        hj_scales = keep.tile([P, GRAPHS * GROUP], U8, align_bytes=64)
+
+        def spread_h(g):
+            nodes = slice(g * I_OF_GROUP, (g + 1) * I_OF_GROUP)
+            nc.vector.tensor_copy(
+                out=hi_codes[:].bitcast(I32).rearrange("p (n j) -> p n j", j=NODES)[:, nodes, :],
+                in_=four_codes[:]
+                .bitcast(I32)
+                .rearrange("p (n w) -> p n w", w=WORD_BYTES)[:, nodes, 0:1]
+                .to_broadcast([P, I_OF_GROUP, NODES]),
+            )
+            nc.vector.tensor_copy(
+                out=hi_scales[:].bitcast(I32).rearrange("p (n w) -> p n w", w=NODES // WORD_BYTES)[:, nodes, :],
+                in_=four_scales[:]
+                .bitcast(I32)[:, nodes]
+                .unsqueeze(2)
+                .to_broadcast([P, I_OF_GROUP, NODES // WORD_BYTES]),
+            )
+            if g % 2 == 0:
+                b = g // 2
+                nc.vector.tensor_copy(
+                    out=hj_codes[:].bitcast(I32)[:, b * GROUP : (b + 1) * GROUP].rearrange("p (i j) -> p i j", j=NODES),
+                    in_=once_codes[:]
+                    .bitcast(I32)[:, b * NODES : (b + 1) * NODES]
+                    .unsqueeze(1)
+                    .to_broadcast([P, I_OF_GROUP, NODES]),
+                )
+                words = NODES // WORD_BYTES
+                nc.vector.tensor_copy(
+                    out=hj_scales[:]
+                    .bitcast(I32)[:, b * I_OF_GROUP * words : (b + 1) * I_OF_GROUP * words]
+                    .rearrange("p (i w) -> p i w", w=words),
+                    in_=once_scales[:]
+                    .bitcast(I32)[:, b * words : (b + 1) * words]
+                    .unsqueeze(1)
+                    .to_broadcast([P, I_OF_GROUP, words]),
+                )
+
+        b1_wide = keep.tile([P, P], F32)
+        nc.vector.tensor_copy(out=b1_wide[:], in_=b1_rows[:])
+        b1_flip = flip_banks.tile([P, P], F32, tag="flip")
+        nc.tensor.transpose(b1_flip[:], b1_wide[:], ident[:])
+        b1_col = keep.tile([P, PACK], F32)
+        nc.vector.tensor_copy(out=b1_col[:], in_=b1_flip[:, 0:PACK])
+
+        w_codes = []
+        w_scales = []
+
+        def quantise_weights(blk):
+            grouped = stage.tile([P, D * PACK], BF16, align_bytes=64, tag="w_grouped")
+            copy = nc.vector.tensor_copy if blk % 2 == 0 else nc.scalar.copy
+            copy(
+                out=grouped[:].rearrange("p (c t) -> p c t", t=PACK),
+                in_=w_raw[blk][:].rearrange("p (t c) -> p c t", t=PACK),
+            )
+            codes = keep.tile([P, D], U32, align_bytes=64, name="w_codes%d" % blk)
+            scales = keep.tile([P, D], U8, align_bytes=64, name="w_scales%d" % blk)
+            nc.vector.quantize_mx(out=codes[:].bitcast(FP8X4), scales=scales[:], in_=grouped[:])
+            w_codes.append(codes)
+            w_scales.append(scales)
+
+        ef_q = {}
+        u_plain = {}
+        u_q = {}
+        res = {}
+
+        def quantise_edges(g):
+            words = ef_sb[g][:].bitcast(F32)
+            grouped = stage.tile([P, GROUP * PACK], BF16, align_bytes=64, tag="ef_grouped")
+            grouped_words = grouped[:].bitcast(F32).rearrange("p (r n u) -> p r n u", r=ROWS, u=2)
+            flips = []
+            for half in range(2):
+                flip = flip_banks.tile([P, 2, 2, P], F32, tag="flip")
+                for rr in range(2):
+                    for u in range(2):
+                        first = ((2 * half + rr) * 2 + u) * P
+                        nc.tensor.transpose(flip[:, rr, u, :], words[:, first : first + P], ident[:])
+                flips.append(flip)
+            for half in range(2):
+                nc.scalar.copy(
+                    out=grouped_words[:, 2 * half : 2 * half + 2],
+                    in_=flips[half][:].rearrange("p r u n -> p r n u"),
+                )
+            codes = stage.tile([P, GROUP], U32, align_bytes=64, tag="ef_codes")
+            scales = stage.tile([P, GROUP], U8, align_bytes=64, tag="ef_scales")
+            nc.vector.quantize_mx(out=codes[:].bitcast(FP8X4), scales=scales[:], in_=grouped[:])
+            ef_q[g] = (codes, scales)
+
+        def residual(g):
+            res_g = results.tile([P, ROWS, D], F32, tag="res")
+            nc.vector.tensor_tensor(
+                out=res_g[:],
+                in0=ef_sb[g][:].rearrange("p (r d) -> p r d", r=ROWS),
+                in1=b2_all[:].unsqueeze(1).to_broadcast([P, ROWS, D]),
+                op=ADD,
+            )
+            res[g] = res_g
+
+        def first_layer(g):
+            b = g // 2
+            moving = (
+                (hi_codes[:, g * GROUP : (g + 1) * GROUP], hi_scales[:, g * GROUP : (g + 1) * GROUP]),
+                (hj_codes[:, b * GROUP : (b + 1) * GROUP], hj_scales[:, b * GROUP : (b + 1) * GROUP]),
+                (ef_q[g][0][:], ef_q[g][1][:]),
+            )
+            u_g = stage.tile([P, PACK, GROUP], BF16, tag="u_plain")
+            for t in range(PACK):
+                chunk = slice(t * P, (t + 1) * P)
+                pre = mx_banks.tile([P, GROUP], F32, tag="mx")
+                for blk in range(3):
+                    nc.tensor.matmul_mx(
+                        out=pre[:],
+                        lhsT=w_codes[blk][:, chunk].bitcast(FP8X4),
+                        lhsT_scale=w_scales[blk][:, chunk],
+                        rhs=moving[blk][0].bitcast(FP8X4),
+                        rhs_scale=moving[blk][1],
+                        start=(blk == 0),
+                        stop=(blk == 2),
+                    )
+                nc.scalar.activation(out=u_g[:, t, :], in_=pre[:], func=GELU, bias=b1_col[:, t : t + 1], scale=1.0)
+            u_plain[g] = u_g
+
+        def quantise_u(g):
+            grouped = stage.tile([P, GROUP * PACK], BF16, align_bytes=64, tag="u_grouped")
+            nc.scalar.copy(
+                out=grouped[:].rearrange("p (n t) -> p n t", t=PACK),
+                in_=u_plain[g][:].rearrange("p t n -> p n t"),
+            )
+            codes = stage.tile([P, GROUP], U32, align_bytes=64, tag="u_codes")
+            scales = stage.tile([P, GROUP], U8, align_bytes=64, tag="u_scales")
+            nc.vector.quantize_mx(out=codes[:].bitcast(FP8X4), scales=scales[:], in_=grouped[:])
+            u_q[g] = (codes, scales)
+
+        def second_layer(g):
+            codes, scales = u_q[g]
+            for r in range(ROWS):
+                edges = slice(r * P, (r + 1) * P)
+                prod = mx_banks.tile([P, D], F32, tag="mx")
+                nc.tensor.matmul_mx(
+                    out=prod[:],
+                    lhsT=codes[:, edges].bitcast(FP8X4),
+                    lhsT_scale=scales[:, edges],
+                    rhs=w_codes[3][:].bitcast(FP8X4),
+                    rhs_scale=w_scales[3][:],
+                    start=True,
+                    stop=True,
+                )
+                nc.vector.tensor_tensor(out=res[g][:, r, :], in0=prod[:], in1=res[g][:, r, :], op=ADD)
+            nc.sync.dma_start(
+                out=out_rows[g * GROUP : (g + 1) * GROUP, :].rearrange("(r p) d -> p r d", p=P),
+                in_=res[g][:],
+            )
+
+        for blk in range(3):
+            quantise_weights(blk)
+        spread_h(0)
+        quantise_edges(0)
+        quantise_weights(3)
+        for g in range(GROUPS):
+            if g + 1 < GROUPS:
+                spread_h(g + 1)
+                quantise_edges(g + 1)
+            residual(g)
+            first_layer(g)
+            if g > 0:
+                second_layer(g - 1)
+            quantise_u(g)
+        second_layer(GROUPS - 1)

@@ -24,6 +24,8 @@ ROWS = GROUP // P
 I_OF_GROUP = GROUP // NODES
 WORD_BYTES = 4
 
+VECTOR_COLUMNS = 336
+
 FLOPS = 2 * D * D * (2 * GRAPHS * NODES + 2 * EDGES)
 
 
@@ -34,9 +36,9 @@ def tile_graphconvlayer_pb_kernel(tc, h, edge_features, Wu1_w, Wu1_b, Wu2_w, Wu2
     out_rows = out.rearrange("b i j d -> (b i j) d")
 
     with ExitStack() as ctx:
+        ctx.enter_context(tc.manual_schedule())
         keep = ctx.enter_context(tc.tile_pool(name="keep", bufs=1))
         stage = ctx.enter_context(tc.tile_pool(name="stage", bufs=2))
-        results = ctx.enter_context(tc.tile_pool(name="results", bufs=3))
         flip_banks = ctx.enter_context(tc.psum_pool(name="flip_banks", bufs=2))
         mx_banks = ctx.enter_context(tc.psum_pool(name="mx_banks", bufs=6))
 
@@ -44,20 +46,17 @@ def tile_graphconvlayer_pb_kernel(tc, h, edge_features, Wu1_w, Wu1_b, Wu2_w, Wu2
         nc.sync.dma_start(out=h_sb[:], in_=h_rows)
         w_raw = []
         for blk in range(3):
-            raw = keep.tile([P, PACK * D], BF16, name="w_raw%d" % blk)
+            raw = keep.tile([P, PACK, D], BF16, name="w_raw%d" % blk)
             nc.sync.dma_start(
-                out=raw[:].rearrange("p (u e c) -> p u e c", u=2, e=2),
+                out=raw[:].rearrange("p (u e) c -> p u e c", u=2),
                 in_=Wu1_w[blk * D : (blk + 1) * D, :].rearrange("(u p e) c -> p u e c", u=2, e=2),
             )
             w_raw.append(raw)
         ef_sb = []
         for g in range(GROUPS):
-            if g == 1:
-                raw = keep.tile([P, PACK * D], BF16, name="w_raw3")
-                nc.sync.dma_start(
-                    out=raw[:].rearrange("p (t c) -> p t c", t=PACK),
-                    in_=Wu2_w.rearrange("(t p) c -> p t c", p=P),
-                )
+            if g == 2:
+                raw = keep.tile([P, PACK, D], BF16, name="w_raw3")
+                nc.sync.dma_start(out=raw[:], in_=Wu2_w.rearrange("(t p) c -> p t c", p=P))
                 w_raw.append(raw)
             ef_g = keep.tile([P, ROWS * D], BF16, name="ef%d" % g)
             nc.sync.dma_start(
@@ -79,14 +78,30 @@ def tile_graphconvlayer_pb_kernel(tc, h, edge_features, Wu1_w, Wu1_b, Wu2_w, Wu2
         ident = keep.tile([P, P], F32)
         masks.make_identity(nc, ident[:])
 
-        h_flip = flip_banks.tile([P, 2, P], F32, tag="flip")
+        res = []
+        for g in range(GROUPS):
+            res_g = keep.tile([P, ROWS, D], F32, name="res%d" % g)
+            for r in range(ROWS):
+                nc.gpsimd.tensor_tensor(
+                    out=res_g[:, r, :], in0=ef_sb[g][:, r * D : (r + 1) * D], in1=b2_all[:], op=ADD
+                )
+            res.append(res_g)
+
+        def side_by_side(grouped, planes):
+            dst = grouped.rearrange("p (c i t) -> p c t i", i=4, t=PACK)
+            src = planes.rearrange("p t (c i) -> p c t i", i=4)
+            cut = VECTOR_COLUMNS // 4
+            nc.vector.tensor_copy(out=dst[:, 0:cut], in_=src[:, 0:cut])
+            nc.scalar.copy(out=dst[:, cut:], in_=src[:, cut:])
+
+        h_flip = mx_banks.tile([P, 2, P], F32, tag="mx")
         for u in range(2):
             nc.tensor.transpose(h_flip[:, u, :], h_sb[:].bitcast(F32)[:, u * P : (u + 1) * P], ident[:])
         h_flip_nu = h_flip[:].rearrange("p u n -> p n u")
         h_once = keep.tile([P, GRAPHS * NODES * PACK], BF16, align_bytes=64)
         nc.vector.tensor_copy(out=h_once[:].bitcast(F32).rearrange("p (n u) -> p n u", u=2), in_=h_flip_nu)
         h_four = keep.tile([P, GRAPHS * NODES * WORD_BYTES * PACK], BF16, align_bytes=64)
-        nc.vector.tensor_copy(
+        nc.scalar.copy(
             out=h_four[:].bitcast(F32).rearrange("p (n w u) -> p n w u", w=WORD_BYTES, u=2),
             in_=h_flip_nu.unsqueeze(2).to_broadcast([P, GRAPHS * NODES, WORD_BYTES, 2]),
         )
@@ -97,7 +112,6 @@ def tile_graphconvlayer_pb_kernel(tc, h, edge_features, Wu1_w, Wu1_b, Wu2_w, Wu2
         nc.vector.memset(once_scales[:].bitcast(I32), 0)
         nc.vector.memset(four_scales[:].bitcast(I32), 0)
         nc.vector.quantize_mx(out=once_codes[:].bitcast(FP8X4), scales=once_scales[:], in_=h_once[:])
-        nc.vector.quantize_mx(out=four_codes[:].bitcast(FP8X4), scales=four_scales[:], in_=h_four[:])
 
         hi_codes = keep.tile([P, EDGES], U32, align_bytes=64)
         hi_scales = keep.tile([P, EDGES], U8, align_bytes=64)
@@ -106,6 +120,7 @@ def tile_graphconvlayer_pb_kernel(tc, h, edge_features, Wu1_w, Wu1_b, Wu2_w, Wu2
 
         def spread_h(g):
             nodes = slice(g * I_OF_GROUP, (g + 1) * I_OF_GROUP)
+            words = NODES // WORD_BYTES
             nc.vector.tensor_copy(
                 out=hi_codes[:].bitcast(I32).rearrange("p (n j) -> p n j", j=NODES)[:, nodes, :],
                 in_=four_codes[:]
@@ -114,11 +129,8 @@ def tile_graphconvlayer_pb_kernel(tc, h, edge_features, Wu1_w, Wu1_b, Wu2_w, Wu2
                 .to_broadcast([P, I_OF_GROUP, NODES]),
             )
             nc.vector.tensor_copy(
-                out=hi_scales[:].bitcast(I32).rearrange("p (n w) -> p n w", w=NODES // WORD_BYTES)[:, nodes, :],
-                in_=four_scales[:]
-                .bitcast(I32)[:, nodes]
-                .unsqueeze(2)
-                .to_broadcast([P, I_OF_GROUP, NODES // WORD_BYTES]),
+                out=hi_scales[:].bitcast(I32).rearrange("p (n w) -> p n w", w=words)[:, nodes, :],
+                in_=four_scales[:].bitcast(I32)[:, nodes].unsqueeze(2).to_broadcast([P, I_OF_GROUP, words]),
             )
             if g % 2 == 0:
                 b = g // 2
@@ -129,7 +141,6 @@ def tile_graphconvlayer_pb_kernel(tc, h, edge_features, Wu1_w, Wu1_b, Wu2_w, Wu2
                     .unsqueeze(1)
                     .to_broadcast([P, I_OF_GROUP, NODES]),
                 )
-                words = NODES // WORD_BYTES
                 nc.vector.tensor_copy(
                     out=hj_scales[:]
                     .bitcast(I32)[:, b * I_OF_GROUP * words : (b + 1) * I_OF_GROUP * words]
@@ -142,33 +153,33 @@ def tile_graphconvlayer_pb_kernel(tc, h, edge_features, Wu1_w, Wu1_b, Wu2_w, Wu2
 
         b1_wide = keep.tile([P, P], F32)
         nc.vector.tensor_copy(out=b1_wide[:], in_=b1_rows[:])
-        b1_flip = flip_banks.tile([P, P], F32, tag="flip")
+        b1_flip = mx_banks.tile([P, P], F32, tag="mx")
         nc.tensor.transpose(b1_flip[:], b1_wide[:], ident[:])
         b1_col = keep.tile([P, PACK], F32)
-        nc.vector.tensor_copy(out=b1_col[:], in_=b1_flip[:, 0:PACK])
 
+        w_grouped = []
         w_codes = []
         w_scales = []
 
+        def regroup_weights(blk):
+            grouped = keep.tile([P, D * PACK], BF16, align_bytes=64, name="w_grouped%d" % blk)
+            side_by_side(grouped[:], w_raw[blk][:])
+            w_grouped.append(grouped)
+
         def quantise_weights(blk):
-            grouped = stage.tile([P, D * PACK], BF16, align_bytes=64, tag="w_grouped")
-            copy = nc.vector.tensor_copy if blk % 2 == 0 else nc.scalar.copy
-            copy(
-                out=grouped[:].rearrange("p (c t) -> p c t", t=PACK),
-                in_=w_raw[blk][:].rearrange("p (t c) -> p c t", t=PACK),
-            )
             codes = keep.tile([P, D], U32, align_bytes=64, name="w_codes%d" % blk)
             scales = keep.tile([P, D], U8, align_bytes=64, name="w_scales%d" % blk)
-            nc.vector.quantize_mx(out=codes[:].bitcast(FP8X4), scales=scales[:], in_=grouped[:])
+            nc.vector.quantize_mx(out=codes[:].bitcast(FP8X4), scales=scales[:], in_=w_grouped[blk][:])
             w_codes.append(codes)
             w_scales.append(scales)
 
+        ef_grouped = {}
         ef_q = {}
         u_plain = {}
+        u_grouped = {}
         u_q = {}
-        res = {}
 
-        def quantise_edges(g):
+        def flip_edges(g):
             words = ef_sb[g][:].bitcast(F32)
             grouped = stage.tile([P, GROUP * PACK], BF16, align_bytes=64, tag="ef_grouped")
             grouped_words = grouped[:].bitcast(F32).rearrange("p (r n u) -> p r n u", r=ROWS, u=2)
@@ -185,20 +196,13 @@ def tile_graphconvlayer_pb_kernel(tc, h, edge_features, Wu1_w, Wu1_b, Wu2_w, Wu2
                     out=grouped_words[:, 2 * half : 2 * half + 2],
                     in_=flips[half][:].rearrange("p r u n -> p r n u"),
                 )
+            ef_grouped[g] = grouped
+
+        def quantise_edges(g):
             codes = stage.tile([P, GROUP], U32, align_bytes=64, tag="ef_codes")
             scales = stage.tile([P, GROUP], U8, align_bytes=64, tag="ef_scales")
-            nc.vector.quantize_mx(out=codes[:].bitcast(FP8X4), scales=scales[:], in_=grouped[:])
+            nc.vector.quantize_mx(out=codes[:].bitcast(FP8X4), scales=scales[:], in_=ef_grouped[g][:])
             ef_q[g] = (codes, scales)
-
-        def residual(g):
-            res_g = results.tile([P, ROWS, D], F32, tag="res")
-            nc.vector.tensor_tensor(
-                out=res_g[:],
-                in0=ef_sb[g][:].rearrange("p (r d) -> p r d", r=ROWS),
-                in1=b2_all[:].unsqueeze(1).to_broadcast([P, ROWS, D]),
-                op=ADD,
-            )
-            res[g] = res_g
 
         def first_layer(g):
             b = g // 2
@@ -224,15 +228,15 @@ def tile_graphconvlayer_pb_kernel(tc, h, edge_features, Wu1_w, Wu1_b, Wu2_w, Wu2
                 nc.scalar.activation(out=u_g[:, t, :], in_=pre[:], func=GELU, bias=b1_col[:, t : t + 1], scale=1.0)
             u_plain[g] = u_g
 
-        def quantise_u(g):
+        def regroup_u(g):
             grouped = stage.tile([P, GROUP * PACK], BF16, align_bytes=64, tag="u_grouped")
-            nc.scalar.copy(
-                out=grouped[:].rearrange("p (n t) -> p n t", t=PACK),
-                in_=u_plain[g][:].rearrange("p t n -> p n t"),
-            )
+            side_by_side(grouped[:], u_plain[g][:])
+            u_grouped[g] = grouped
+
+        def quantise_u(g):
             codes = stage.tile([P, GROUP], U32, align_bytes=64, tag="u_codes")
             scales = stage.tile([P, GROUP], U8, align_bytes=64, tag="u_scales")
-            nc.vector.quantize_mx(out=codes[:].bitcast(FP8X4), scales=scales[:], in_=grouped[:])
+            nc.vector.quantize_mx(out=codes[:].bitcast(FP8X4), scales=scales[:], in_=u_grouped[g][:])
             u_q[g] = (codes, scales)
 
         def second_layer(g):
@@ -255,18 +259,32 @@ def tile_graphconvlayer_pb_kernel(tc, h, edge_features, Wu1_w, Wu1_b, Wu2_w, Wu2
                 in_=res[g][:],
             )
 
-        for blk in range(3):
-            quantise_weights(blk)
+        regroup_weights(0)
+        nc.vector.quantize_mx(out=four_codes[:].bitcast(FP8X4), scales=four_scales[:], in_=h_four[:])
+        regroup_weights(1)
         spread_h(0)
+        quantise_weights(0)
+        regroup_weights(2)
+        quantise_weights(1)
+        nc.vector.tensor_copy(out=b1_col[:], in_=b1_flip[:, 0:PACK])
+        flip_edges(0)
+        quantise_weights(2)
         quantise_edges(0)
-        quantise_weights(3)
-        for g in range(GROUPS):
-            if g + 1 < GROUPS:
-                spread_h(g + 1)
-                quantise_edges(g + 1)
-            residual(g)
-            first_layer(g)
-            if g > 0:
-                second_layer(g - 1)
-            quantise_u(g)
-        second_layer(GROUPS - 1)
+
+        for r in range(GROUPS + 1):
+            if r >= 1:
+                quantise_u(r - 1)
+            if r + 1 < GROUPS:
+                flip_edges(r + 1)
+                spread_h(r + 1)
+                quantise_edges(r + 1)
+            if r == 0:
+                regroup_weights(3)
+            if r < GROUPS:
+                first_layer(r)
+            if r == 0:
+                quantise_weights(3)
+            if r >= 1:
+                second_layer(r - 1)
+            if r < GROUPS:
+                regroup_u(r)

@@ -39,6 +39,7 @@ def tile_graphconvlayer_pb_kernel(tc, h, edge_features, Wu1_w, Wu1_b, Wu2_w, Wu2
         ctx.enter_context(tc.manual_schedule())
         keep = ctx.enter_context(tc.tile_pool(name="keep", bufs=1))
         stage = ctx.enter_context(tc.tile_pool(name="stage", bufs=2))
+        results = ctx.enter_context(tc.tile_pool(name="results", bufs=4))
         flip_banks = ctx.enter_context(tc.psum_pool(name="flip_banks", bufs=2))
         mx_banks = ctx.enter_context(tc.psum_pool(name="mx_banks", bufs=6))
 
@@ -78,21 +79,11 @@ def tile_graphconvlayer_pb_kernel(tc, h, edge_features, Wu1_w, Wu1_b, Wu2_w, Wu2
         ident = keep.tile([P, P], F32)
         masks.make_identity(nc, ident[:])
 
-        res = []
-        for g in range(GROUPS):
-            res_g = keep.tile([P, ROWS, D], F32, name="res%d" % g)
-            for r in range(ROWS):
-                nc.gpsimd.tensor_tensor(
-                    out=res_g[:, r, :], in0=ef_sb[g][:, r * D : (r + 1) * D], in1=b2_all[:], op=ADD
-                )
-            res.append(res_g)
 
-        def side_by_side(grouped, planes):
+        def side_by_side_views(grouped, planes):
             dst = grouped.rearrange("p (c i t) -> p c t i", i=4, t=PACK)
             src = planes.rearrange("p t (c i) -> p c t i", i=4)
-            cut = VECTOR_COLUMNS // 4
-            nc.vector.tensor_copy(out=dst[:, 0:cut], in_=src[:, 0:cut])
-            nc.scalar.copy(out=dst[:, cut:], in_=src[:, cut:])
+            return dst, src
 
         h_flip = mx_banks.tile([P, 2, P], F32, tag="mx")
         for u in range(2):
@@ -163,7 +154,10 @@ def tile_graphconvlayer_pb_kernel(tc, h, edge_features, Wu1_w, Wu1_b, Wu2_w, Wu2
 
         def regroup_weights(blk):
             grouped = keep.tile([P, D * PACK], BF16, align_bytes=64, name="w_grouped%d" % blk)
-            side_by_side(grouped[:], w_raw[blk][:])
+            dst, src = side_by_side_views(grouped[:], w_raw[blk][:])
+            cut = VECTOR_COLUMNS // 4
+            nc.vector.tensor_copy(out=dst[:, 0:cut], in_=src[:, 0:cut])
+            nc.scalar.copy(out=dst[:, cut:], in_=src[:, cut:])
             w_grouped.append(grouped)
 
         def quantise_weights(blk):
@@ -178,6 +172,7 @@ def tile_graphconvlayer_pb_kernel(tc, h, edge_features, Wu1_w, Wu1_b, Wu2_w, Wu2
         u_plain = {}
         u_grouped = {}
         u_q = {}
+        res = {}
 
         def flip_edges(g):
             words = ef_sb[g][:].bitcast(F32)
@@ -203,6 +198,16 @@ def tile_graphconvlayer_pb_kernel(tc, h, edge_features, Wu1_w, Wu1_b, Wu2_w, Wu2
             scales = stage.tile([P, GROUP], U8, align_bytes=64, tag="ef_scales")
             nc.vector.quantize_mx(out=codes[:].bitcast(FP8X4), scales=scales[:], in_=ef_grouped[g][:])
             ef_q[g] = (codes, scales)
+
+        def residual(g):
+            res_g = results.tile([P, ROWS, D], F32, tag="res")
+            nc.vector.tensor_tensor(
+                out=res_g[:],
+                in0=ef_sb[g][:].rearrange("p (r d) -> p r d", r=ROWS),
+                in1=b2_all[:].unsqueeze(1).to_broadcast([P, ROWS, D]),
+                op=ADD,
+            )
+            res[g] = res_g
 
         def first_layer(g):
             b = g // 2
@@ -230,7 +235,8 @@ def tile_graphconvlayer_pb_kernel(tc, h, edge_features, Wu1_w, Wu1_b, Wu2_w, Wu2
 
         def regroup_u(g):
             grouped = stage.tile([P, GROUP * PACK], BF16, align_bytes=64, tag="u_grouped")
-            side_by_side(grouped[:], u_plain[g][:])
+            dst, src = side_by_side_views(grouped[:], u_plain[g][:])
+            nc.scalar.copy(out=dst, in_=src)
             u_grouped[g] = grouped
 
         def quantise_u(g):
@@ -281,6 +287,7 @@ def tile_graphconvlayer_pb_kernel(tc, h, edge_features, Wu1_w, Wu1_b, Wu2_w, Wu2
             if r == 0:
                 regroup_weights(3)
             if r < GROUPS:
+                residual(r)
                 first_layer(r)
             if r == 0:
                 quantise_weights(3)

@@ -25,6 +25,8 @@ I_OF_GROUP = GROUP // NODES
 WORD_BYTES = 4
 
 VECTOR_COLUMNS = 336
+VECTOR_ROWS = 2
+GPSIMD_PIECE = 128
 
 FLOPS = 2 * D * D * (2 * GRAPHS * NODES + 2 * EDGES)
 
@@ -201,12 +203,17 @@ def tile_graphconvlayer_pb_kernel(tc, h, edge_features, Wu1_w, Wu1_b, Wu2_w, Wu2
 
         def residual(g):
             res_g = results.tile([P, ROWS, D], F32, tag="res")
+            ef_g = ef_sb[g][:].rearrange("p (r d) -> p r d", r=ROWS)
             nc.vector.tensor_tensor(
-                out=res_g[:],
-                in0=ef_sb[g][:].rearrange("p (r d) -> p r d", r=ROWS),
-                in1=b2_all[:].unsqueeze(1).to_broadcast([P, ROWS, D]),
+                out=res_g[:, 0:VECTOR_ROWS, :],
+                in0=ef_g[:, 0:VECTOR_ROWS, :],
+                in1=b2_all[:].unsqueeze(1).to_broadcast([P, VECTOR_ROWS, D]),
                 op=ADD,
             )
+            for r in range(VECTOR_ROWS, ROWS):
+                for first in range(0, D, GPSIMD_PIECE):
+                    piece = slice(first, first + GPSIMD_PIECE)
+                    nc.gpsimd.tensor_tensor(out=res_g[:, r, piece], in0=ef_g[:, r, piece], in1=b2_all[:, piece], op=ADD)
             res[g] = res_g
 
         def first_layer(g):
@@ -260,10 +267,7 @@ def tile_graphconvlayer_pb_kernel(tc, h, edge_features, Wu1_w, Wu1_b, Wu2_w, Wu2
                     stop=True,
                 )
                 nc.vector.tensor_tensor(out=res[g][:, r, :], in0=prod[:], in1=res[g][:, r, :], op=ADD)
-            nc.sync.dma_start(
-                out=out_rows[g * GROUP : (g + 1) * GROUP, :].rearrange("(r p) d -> p r d", p=P),
-                in_=res[g][:],
-            )
+                nc.sync.dma_start(out=out_rows[g * GROUP + r * P : g * GROUP + (r + 1) * P, :], in_=res[g][:, r, :])
 
         regroup_weights(0)
         nc.vector.quantize_mx(out=four_codes[:].bitcast(FP8X4), scales=four_scales[:], in_=h_four[:])

@@ -23,10 +23,9 @@ GROUPS = EDGES // GROUP
 ROWS = GROUP // P
 I_OF_GROUP = GROUP // NODES
 WORD_BYTES = 4
+RUN = 4
 
 VECTOR_COLUMNS = 336
-VECTOR_ROWS = 2
-GPSIMD_PIECE = 128
 
 FLOPS = 2 * D * D * (2 * GRAPHS * NODES + 2 * EDGES)
 
@@ -81,10 +80,9 @@ def tile_graphconvlayer_pb_kernel(tc, h, edge_features, Wu1_w, Wu1_b, Wu2_w, Wu2
         ident = keep.tile([P, P], F32)
         masks.make_identity(nc, ident[:])
 
-
         def side_by_side_views(grouped, planes):
-            dst = grouped.rearrange("p (c i t) -> p c t i", i=4, t=PACK)
-            src = planes.rearrange("p t (c i) -> p c t i", i=4)
+            dst = grouped.rearrange("p (c i t) -> p c t i", i=RUN, t=PACK)
+            src = planes.rearrange("p t (c i) -> p c t i", i=RUN)
             return dst, src
 
         h_flip = mx_banks.tile([P, 2, P], F32, tag="mx")
@@ -111,38 +109,37 @@ def tile_graphconvlayer_pb_kernel(tc, h, edge_features, Wu1_w, Wu1_b, Wu2_w, Wu2
         hj_codes = keep.tile([P, GRAPHS * GROUP], U32, align_bytes=64)
         hj_scales = keep.tile([P, GRAPHS * GROUP], U8, align_bytes=64)
 
-        def spread_h(g):
-            nodes = slice(g * I_OF_GROUP, (g + 1) * I_OF_GROUP)
+        def spread_h(first, count):
             words = NODES // WORD_BYTES
+            graphs = slice(first, first + count)
+            nodes = slice(first * NODES, (first + count) * NODES)
             nc.vector.tensor_copy(
                 out=hi_codes[:].bitcast(I32).rearrange("p (n j) -> p n j", j=NODES)[:, nodes, :],
                 in_=four_codes[:]
                 .bitcast(I32)
                 .rearrange("p (n w) -> p n w", w=WORD_BYTES)[:, nodes, 0:1]
-                .to_broadcast([P, I_OF_GROUP, NODES]),
+                .to_broadcast([P, count * NODES, NODES]),
             )
             nc.vector.tensor_copy(
                 out=hi_scales[:].bitcast(I32).rearrange("p (n w) -> p n w", w=words)[:, nodes, :],
-                in_=four_scales[:].bitcast(I32)[:, nodes].unsqueeze(2).to_broadcast([P, I_OF_GROUP, words]),
+                in_=four_scales[:].bitcast(I32)[:, nodes].unsqueeze(2).to_broadcast([P, count * NODES, words]),
             )
-            if g % 2 == 0:
-                b = g // 2
-                nc.vector.tensor_copy(
-                    out=hj_codes[:].bitcast(I32)[:, b * GROUP : (b + 1) * GROUP].rearrange("p (i j) -> p i j", j=NODES),
-                    in_=once_codes[:]
-                    .bitcast(I32)[:, b * NODES : (b + 1) * NODES]
-                    .unsqueeze(1)
-                    .to_broadcast([P, I_OF_GROUP, NODES]),
-                )
-                nc.vector.tensor_copy(
-                    out=hj_scales[:]
-                    .bitcast(I32)[:, b * I_OF_GROUP * words : (b + 1) * I_OF_GROUP * words]
-                    .rearrange("p (i w) -> p i w", w=words),
-                    in_=once_scales[:]
-                    .bitcast(I32)[:, b * words : (b + 1) * words]
-                    .unsqueeze(1)
-                    .to_broadcast([P, I_OF_GROUP, words]),
-                )
+            nc.vector.tensor_copy(
+                out=hj_codes[:].bitcast(I32).rearrange("p (b i j) -> p b i j", i=I_OF_GROUP, j=NODES)[:, graphs],
+                in_=once_codes[:]
+                .bitcast(I32)
+                .rearrange("p (b j) -> p b j", j=NODES)[:, graphs]
+                .unsqueeze(2)
+                .to_broadcast([P, count, I_OF_GROUP, NODES]),
+            )
+            nc.vector.tensor_copy(
+                out=hj_scales[:].bitcast(I32).rearrange("p (b i w) -> p b i w", i=I_OF_GROUP, w=words)[:, graphs],
+                in_=once_scales[:]
+                .bitcast(I32)
+                .rearrange("p (b w) -> p b w", w=words)[:, graphs]
+                .unsqueeze(2)
+                .to_broadcast([P, count, I_OF_GROUP, words]),
+            )
 
         b1_wide = keep.tile([P, P], F32)
         nc.vector.tensor_copy(out=b1_wide[:], in_=b1_rows[:])
@@ -157,7 +154,7 @@ def tile_graphconvlayer_pb_kernel(tc, h, edge_features, Wu1_w, Wu1_b, Wu2_w, Wu2
         def regroup_weights(blk):
             grouped = keep.tile([P, D * PACK], BF16, align_bytes=64, name="w_grouped%d" % blk)
             dst, src = side_by_side_views(grouped[:], w_raw[blk][:])
-            cut = VECTOR_COLUMNS // 4
+            cut = VECTOR_COLUMNS // RUN
             nc.vector.tensor_copy(out=dst[:, 0:cut], in_=src[:, 0:cut])
             nc.scalar.copy(out=dst[:, cut:], in_=src[:, cut:])
             w_grouped.append(grouped)
@@ -203,17 +200,12 @@ def tile_graphconvlayer_pb_kernel(tc, h, edge_features, Wu1_w, Wu1_b, Wu2_w, Wu2
 
         def residual(g):
             res_g = results.tile([P, ROWS, D], F32, tag="res")
-            ef_g = ef_sb[g][:].rearrange("p (r d) -> p r d", r=ROWS)
             nc.vector.tensor_tensor(
-                out=res_g[:, 0:VECTOR_ROWS, :],
-                in0=ef_g[:, 0:VECTOR_ROWS, :],
-                in1=b2_all[:].unsqueeze(1).to_broadcast([P, VECTOR_ROWS, D]),
+                out=res_g[:],
+                in0=ef_sb[g][:].rearrange("p (r d) -> p r d", r=ROWS),
+                in1=b2_all[:].unsqueeze(1).to_broadcast([P, ROWS, D]),
                 op=ADD,
             )
-            for r in range(VECTOR_ROWS, ROWS):
-                for first in range(0, D, GPSIMD_PIECE):
-                    piece = slice(first, first + GPSIMD_PIECE)
-                    nc.gpsimd.tensor_tensor(out=res_g[:, r, piece], in0=ef_g[:, r, piece], in1=b2_all[:, piece], op=ADD)
             res[g] = res_g
 
         def first_layer(g):
@@ -272,7 +264,7 @@ def tile_graphconvlayer_pb_kernel(tc, h, edge_features, Wu1_w, Wu1_b, Wu2_w, Wu2
         regroup_weights(0)
         nc.vector.quantize_mx(out=four_codes[:].bitcast(FP8X4), scales=four_scales[:], in_=h_four[:])
         regroup_weights(1)
-        spread_h(0)
+        spread_h(0, 1)
         quantise_weights(0)
         regroup_weights(2)
         quantise_weights(1)
@@ -286,7 +278,6 @@ def tile_graphconvlayer_pb_kernel(tc, h, edge_features, Wu1_w, Wu1_b, Wu2_w, Wu2
                 quantise_u(r - 1)
             if r + 1 < GROUPS:
                 flip_edges(r + 1)
-                spread_h(r + 1)
                 quantise_edges(r + 1)
             if r == 0:
                 regroup_weights(3)
@@ -295,6 +286,7 @@ def tile_graphconvlayer_pb_kernel(tc, h, edge_features, Wu1_w, Wu1_b, Wu2_w, Wu2
                 first_layer(r)
             if r == 0:
                 quantise_weights(3)
+                spread_h(1, GRAPHS - 1)
             if r >= 1:
                 second_layer(r - 1)
             if r < GROUPS:

@@ -70,8 +70,11 @@ def tile_graphconvlayer_pb_kernel(tc, h, edge_features, Wu1_w, Wu1_b, Wu2_w, Wu2
         b1_rows = keep.tile([P, P], BF16)
         nc.vector.memset(b1_rows[:], 0.0)
         nc.scalar.dma_start(out=b1_rows[0:PACK, :], in_=Wu1_b.rearrange("(t p) -> t p", p=P))
-        b2_all = keep.tile([P, D], BF16)
-        nc.scalar.dma_start(out=b2_all[:], in_=Wu2_b.partition_broadcast(P))
+        b2_row = keep.tile([P, D], BF16)
+        nc.vector.memset(b2_row[:], 0.0)
+        nc.scalar.dma_start(out=b2_row[0:1, :], in_=Wu2_b.rearrange("(o d) -> o d", o=1))
+        ones = keep.tile([P, P], BF16)
+        nc.vector.memset(ones[:], 1.0)
 
         warm = keep.tile([P, 1], F32)
         nc.vector.memset(warm[:], 0.0)
@@ -146,6 +149,11 @@ def tile_graphconvlayer_pb_kernel(tc, h, edge_features, Wu1_w, Wu1_b, Wu2_w, Wu2
         b1_flip = mx_banks.tile([P, P], F32, tag="mx")
         nc.tensor.transpose(b1_flip[:], b1_wide[:], ident[:])
         b1_col = keep.tile([P, PACK], F32)
+
+        b2_bank = mx_banks.tile([P, D], F32, tag="mx")
+        nc.tensor.matmul(out=b2_bank[:], lhsT=ones[:], rhs=b2_row[:], start=True, stop=True)
+        b2_all = keep.tile([P, D], BF16)
+        nc.scalar.copy(out=b2_all[:], in_=b2_bank[:])
 
         w_grouped = []
         w_codes = []

@@ -88,6 +88,12 @@ def tile_graphconvlayer_pb_kernel(tc, h, edge_features, Wu1_w, Wu1_b, Wu2_w, Wu2
             src = planes.rearrange("p t (c i) -> p c t i", i=RUN)
             return dst, src
 
+        once_codes = keep.tile([P, GRAPHS * NODES], U32, align_bytes=64)
+        once_scales = keep.tile([P, GRAPHS * NODES], U8, align_bytes=64)
+        four_codes = keep.tile([P, GRAPHS * NODES * WORD_BYTES], U32, align_bytes=64)
+        four_scales = keep.tile([P, GRAPHS * NODES * WORD_BYTES], U8, align_bytes=64)
+        nc.vector.memset(once_scales[:].bitcast(I32), 0)
+        nc.vector.memset(four_scales[:].bitcast(I32), 0)
         h_flip = mx_banks.tile([P, 2, P], F32, tag="mx")
         for u in range(2):
             nc.tensor.transpose(h_flip[:, u, :], h_sb[:].bitcast(F32)[:, u * P : (u + 1) * P], ident[:])
@@ -99,12 +105,6 @@ def tile_graphconvlayer_pb_kernel(tc, h, edge_features, Wu1_w, Wu1_b, Wu2_w, Wu2
             out=h_four[:].bitcast(F32).rearrange("p (n w u) -> p n w u", w=WORD_BYTES, u=2),
             in_=h_flip_nu.unsqueeze(2).to_broadcast([P, GRAPHS * NODES, WORD_BYTES, 2]),
         )
-        once_codes = keep.tile([P, GRAPHS * NODES], U32, align_bytes=64)
-        once_scales = keep.tile([P, GRAPHS * NODES], U8, align_bytes=64)
-        four_codes = keep.tile([P, GRAPHS * NODES * WORD_BYTES], U32, align_bytes=64)
-        four_scales = keep.tile([P, GRAPHS * NODES * WORD_BYTES], U8, align_bytes=64)
-        nc.vector.memset(once_scales[:].bitcast(I32), 0)
-        nc.vector.memset(four_scales[:].bitcast(I32), 0)
         nc.vector.quantize_mx(out=once_codes[:].bitcast(FP8X4), scales=once_scales[:], in_=h_once[:])
 
         hi_codes = keep.tile([P, EDGES], U32, align_bytes=64)
@@ -143,17 +143,6 @@ def tile_graphconvlayer_pb_kernel(tc, h, edge_features, Wu1_w, Wu1_b, Wu2_w, Wu2
                 .unsqueeze(2)
                 .to_broadcast([P, count, I_OF_GROUP, words]),
             )
-
-        b1_wide = keep.tile([P, P], F32)
-        nc.vector.tensor_copy(out=b1_wide[:], in_=b1_rows[:])
-        b1_flip = mx_banks.tile([P, P], F32, tag="mx")
-        nc.tensor.transpose(b1_flip[:], b1_wide[:], ident[:])
-        b1_col = keep.tile([P, PACK], F32)
-
-        b2_bank = mx_banks.tile([P, D], F32, tag="mx")
-        nc.tensor.matmul(out=b2_bank[:], lhsT=ones[:], rhs=b2_row[:], start=True, stop=True)
-        b2_all = keep.tile([P, D], BF16)
-        nc.scalar.copy(out=b2_all[:], in_=b2_bank[:])
 
         w_grouped = []
         w_codes = []
@@ -276,9 +265,18 @@ def tile_graphconvlayer_pb_kernel(tc, h, edge_features, Wu1_w, Wu1_b, Wu2_w, Wu2
         quantise_weights(0)
         regroup_weights(2)
         quantise_weights(1)
-        nc.vector.tensor_copy(out=b1_col[:], in_=b1_flip[:, 0:PACK])
         flip_edges(0)
+        b1_wide = keep.tile([P, P], F32)
+        nc.vector.tensor_copy(out=b1_wide[:], in_=b1_rows[:])
+        b1_flip = mx_banks.tile([P, P], F32, tag="mx")
+        nc.tensor.transpose(b1_flip[:], b1_wide[:], ident[:])
         quantise_weights(2)
+        b1_col = keep.tile([P, PACK], F32)
+        nc.vector.tensor_copy(out=b1_col[:], in_=b1_flip[:, 0:PACK])
+        b2_bank = mx_banks.tile([P, D], F32, tag="mx")
+        nc.tensor.matmul(out=b2_bank[:], lhsT=ones[:], rhs=b2_row[:], start=True, stop=True)
+        b2_all = keep.tile([P, D], BF16)
+        nc.scalar.copy(out=b2_all[:], in_=b2_bank[:])
         quantise_edges(0)
 
         for r in range(GROUPS + 1):

@@ -27,6 +27,8 @@ RUN = 4
 
 VECTOR_COLUMNS = 336
 
+VECTOR_ROWS = 2
+
 FLOPS = 2 * D * D * (2 * GRAPHS * NODES + 2 * EDGES)
 
 
@@ -182,8 +184,8 @@ def tile_graphconvlayer_pb_kernel(tc, h, edge_features, Wu1_w, Wu1_b, Wu2_w, Wu2
                         first = ((2 * half + rr) * 2 + u) * P
                         nc.tensor.transpose(flip[:, rr, u, :], words[:, first : first + P], ident[:])
                 flips.append(flip)
-            for half in range(2):
-                nc.scalar.copy(
+            for half, copy in enumerate((nc.scalar.copy, nc.scalar.copy if g < 2 else nc.vector.tensor_copy)):
+                copy(
                     out=grouped_words[:, 2 * half : 2 * half + 2],
                     in_=flips[half][:].rearrange("p r u n -> p r n u"),
                 )
@@ -198,11 +200,14 @@ def tile_graphconvlayer_pb_kernel(tc, h, edge_features, Wu1_w, Wu1_b, Wu2_w, Wu2
         def residual(g):
             res_g = results.tile([P, ROWS, D], F32, tag="res")
             nc.vector.tensor_tensor(
-                out=res_g[:],
-                in0=ef_sb[g][:].rearrange("p (r d) -> p r d", r=ROWS),
-                in1=b2_all[:].unsqueeze(1).to_broadcast([P, ROWS, D]),
+                out=res_g[:, 0:VECTOR_ROWS],
+                in0=ef_sb[g][:].rearrange("p (r d) -> p r d", r=ROWS)[:, 0:VECTOR_ROWS],
+                in1=b2_all[:].unsqueeze(1).to_broadcast([P, VECTOR_ROWS, D]),
                 op=ADD,
             )
+            nc.vector.memset(res_g[:, VECTOR_ROWS, 0:8], 0.0)
+            for r in range(VECTOR_ROWS, ROWS):
+                nc.gpsimd.tensor_tensor(out=res_g[:, r, :], in0=ef_sb[g][:, r * D : (r + 1) * D], in1=b2_all[:], op=ADD)
             res[g] = res_g
 
         def first_layer(g):
@@ -280,19 +285,22 @@ def tile_graphconvlayer_pb_kernel(tc, h, edge_features, Wu1_w, Wu1_b, Wu2_w, Wu2
         quantise_edges(0)
 
         for r in range(GROUPS + 1):
+            if r + 1 < GROUPS:
+                flip_edges(r + 1)
             if r >= 1:
                 quantise_u(r - 1)
             if r + 1 < GROUPS:
-                flip_edges(r + 1)
                 quantise_edges(r + 1)
             if r == 0:
                 regroup_weights(3)
-            if r < GROUPS:
+            if 1 <= r < GROUPS:
                 residual(r)
+            if r < GROUPS:
                 first_layer(r)
             if r == 0:
                 quantise_weights(3)
                 spread_h(1, GRAPHS - 1)
+                residual(0)
             if r >= 1:
                 second_layer(r - 1)
             if r < GROUPS:

@@ -18,16 +18,17 @@ D = P * PACK
 GRAPHS = 4
 NODES = 32
 EDGES = GRAPHS * NODES * NODES
-GROUP = 512
-GROUPS = EDGES // GROUP
-ROWS = GROUP // P
-I_OF_GROUP = GROUP // NODES
+GROUP_ROWS = [2, 4, 4, 4, 4, 4, 4, 4, 2]
+GROUPS = len(GROUP_ROWS)
+FIRST_ROW = [sum(GROUP_ROWS[:g]) for g in range(GROUPS)]
+PAIR = 2 * P
+I_OF_PAIR = PAIR // NODES
+PAIRS_OF_GRAPH = NODES * NODES // PAIR
 WORD_BYTES = 4
 RUN = 4
 
-VECTOR_COLUMNS = 336
+VECTOR_COLUMNS = 272
 
-VECTOR_ROWS = 2
 
 FLOPS = 2 * D * D * (2 * GRAPHS * NODES + 2 * EDGES)
 
@@ -48,26 +49,38 @@ def tile_graphconvlayer_pb_kernel(tc, h, edge_features, Wu1_w, Wu1_b, Wu2_w, Wu2
 
         h_sb = keep.tile([P, D], BF16)
         nc.sync.dma_start(out=h_sb[:], in_=h_rows)
-        w_raw = []
-        for blk in range(3):
+        w_raw = {}
+        ef_sb = {}
+
+        def load_weights(blk):
             raw = keep.tile([P, PACK, D], BF16, name="w_raw%d" % blk)
-            nc.sync.dma_start(
-                out=raw[:].rearrange("p (u e) c -> p u e c", u=2),
-                in_=Wu1_w[blk * D : (blk + 1) * D, :].rearrange("(u p e) c -> p u e c", u=2, e=2),
-            )
-            w_raw.append(raw)
-        ef_sb = []
-        for g in range(GROUPS):
-            if g == 2:
-                raw = keep.tile([P, PACK, D], BF16, name="w_raw3")
+            if blk == 3:
                 nc.sync.dma_start(out=raw[:], in_=Wu2_w.rearrange("(t p) c -> p t c", p=P))
-                w_raw.append(raw)
-            ef_g = keep.tile([P, ROWS * D], BF16, name="ef%d" % g)
+            else:
+                nc.sync.dma_start(
+                    out=raw[:].rearrange("p (u e) c -> p u e c", u=2),
+                    in_=Wu1_w[blk * D : (blk + 1) * D, :].rearrange("(u p e) c -> p u e c", u=2, e=2),
+                )
+            w_raw[blk] = raw
+
+        def load_edges(g):
+            rows = GROUP_ROWS[g]
+            first = FIRST_ROW[g] * P
+            ef_g = keep.tile([P, rows * D], BF16, name="ef%d" % g)
             nc.sync.dma_start(
-                out=ef_g[:].rearrange("p (r d) -> p r d", r=ROWS),
-                in_=ef_rows[g * GROUP : (g + 1) * GROUP, :].rearrange("(r p) d -> p r d", p=P),
+                out=ef_g[:].rearrange("p (r d) -> p r d", r=rows),
+                in_=ef_rows[first : first + rows * P, :].rearrange("(r p) d -> p r d", p=P),
             )
-            ef_sb.append(ef_g)
+            ef_sb[g] = ef_g
+
+        load_weights(0)
+        load_weights(1)
+        load_edges(0)
+        load_weights(2)
+        load_edges(1)
+        load_weights(3)
+        for g in range(2, GROUPS):
+            load_edges(g)
 
         b1_rows = keep.tile([P, P], BF16)
         nc.vector.memset(b1_rows[:], 0.0)
@@ -111,59 +124,65 @@ def tile_graphconvlayer_pb_kernel(tc, h, edge_features, Wu1_w, Wu1_b, Wu2_w, Wu2
 
         hi_codes = keep.tile([P, EDGES], U32, align_bytes=64)
         hi_scales = keep.tile([P, EDGES], U8, align_bytes=64)
-        hj_codes = keep.tile([P, GRAPHS * GROUP], U32, align_bytes=64)
-        hj_scales = keep.tile([P, GRAPHS * GROUP], U8, align_bytes=64)
+        hj_codes = keep.tile([P, GRAPHS * PAIR], U32, align_bytes=64)
+        hj_scales = keep.tile([P, GRAPHS * PAIR], U8, align_bytes=64)
 
-        def spread_h(first, count):
-            words = NODES // WORD_BYTES
-            graphs = slice(first, first + count)
-            nodes = slice(first * NODES, (first + count) * NODES)
+        words = NODES // WORD_BYTES
+        nodes_of_row = P // NODES
+
+        def spread_hi(g):
+            nodes = slice(FIRST_ROW[g] * nodes_of_row, (FIRST_ROW[g] + GROUP_ROWS[g]) * nodes_of_row)
+            count = GROUP_ROWS[g] * nodes_of_row
             nc.vector.tensor_copy(
                 out=hi_codes[:].bitcast(I32).rearrange("p (n j) -> p n j", j=NODES)[:, nodes, :],
                 in_=four_codes[:]
                 .bitcast(I32)
                 .rearrange("p (n w) -> p n w", w=WORD_BYTES)[:, nodes, 0:1]
-                .to_broadcast([P, count * NODES, NODES]),
+                .to_broadcast([P, count, NODES]),
             )
             nc.vector.tensor_copy(
                 out=hi_scales[:].bitcast(I32).rearrange("p (n w) -> p n w", w=words)[:, nodes, :],
-                in_=four_scales[:].bitcast(I32)[:, nodes].unsqueeze(2).to_broadcast([P, count * NODES, words]),
+                in_=four_scales[:].bitcast(I32)[:, nodes].unsqueeze(2).to_broadcast([P, count, words]),
             )
+
+        def spread_hj(first, count):
+            graphs = slice(first, first + count)
             nc.vector.tensor_copy(
-                out=hj_codes[:].bitcast(I32).rearrange("p (b i j) -> p b i j", i=I_OF_GROUP, j=NODES)[:, graphs],
+                out=hj_codes[:].bitcast(I32).rearrange("p (b i j) -> p b i j", i=I_OF_PAIR, j=NODES)[:, graphs],
                 in_=once_codes[:]
                 .bitcast(I32)
                 .rearrange("p (b j) -> p b j", j=NODES)[:, graphs]
                 .unsqueeze(2)
-                .to_broadcast([P, count, I_OF_GROUP, NODES]),
+                .to_broadcast([P, count, I_OF_PAIR, NODES]),
             )
             nc.vector.tensor_copy(
-                out=hj_scales[:].bitcast(I32).rearrange("p (b i w) -> p b i w", i=I_OF_GROUP, w=words)[:, graphs],
+                out=hj_scales[:].bitcast(I32).rearrange("p (b i w) -> p b i w", i=I_OF_PAIR, w=words)[:, graphs],
                 in_=once_scales[:]
                 .bitcast(I32)
                 .rearrange("p (b w) -> p b w", w=words)[:, graphs]
                 .unsqueeze(2)
-                .to_broadcast([P, count, I_OF_GROUP, words]),
+                .to_broadcast([P, count, I_OF_PAIR, words]),
             )
 
-        w_grouped = []
-        w_codes = []
-        w_scales = []
+        w_grouped = {}
+        w_codes = {}
+        w_scales = {}
 
-        def regroup_weights(blk):
+        def regroup_weights(blk, vector_columns):
             grouped = keep.tile([P, D * PACK], BF16, align_bytes=64, name="w_grouped%d" % blk)
             dst, src = side_by_side_views(grouped[:], w_raw[blk][:])
-            cut = VECTOR_COLUMNS // RUN
+            cut = vector_columns // RUN
             nc.vector.tensor_copy(out=dst[:, 0:cut], in_=src[:, 0:cut])
-            nc.scalar.copy(out=dst[:, cut:], in_=src[:, cut:])
-            w_grouped.append(grouped)
+            if vector_columns < D:
+                nc.scalar.copy(out=dst[:, cut:], in_=src[:, cut:])
+            w_grouped[blk] = grouped
 
         def quantise_weights(blk):
             codes = keep.tile([P, D], U32, align_bytes=64, name="w_codes%d" % blk)
             scales = keep.tile([P, D], U8, align_bytes=64, name="w_scales%d" % blk)
             nc.vector.quantize_mx(out=codes[:].bitcast(FP8X4), scales=scales[:], in_=w_grouped[blk][:])
-            w_codes.append(codes)
-            w_scales.append(scales)
+            w_codes[blk] = codes
+            w_scales[blk] = scales
 
         ef_grouped = {}
         ef_q = {}
@@ -173,18 +192,19 @@ def tile_graphconvlayer_pb_kernel(tc, h, edge_features, Wu1_w, Wu1_b, Wu2_w, Wu2
         res = {}
 
         def flip_edges(g):
-            words = ef_sb[g][:].bitcast(F32)
-            grouped = stage.tile([P, GROUP * PACK], BF16, align_bytes=64, tag="ef_grouped")
-            grouped_words = grouped[:].bitcast(F32).rearrange("p (r n u) -> p r n u", r=ROWS, u=2)
+            rows = GROUP_ROWS[g]
+            words_g = ef_sb[g][:].bitcast(F32)
+            grouped = stage.tile([P, rows * P * PACK], BF16, align_bytes=64, tag="ef_grouped")
+            grouped_words = grouped[:].bitcast(F32).rearrange("p (r n u) -> p r n u", r=rows, u=2)
             flips = []
-            for half in range(2):
+            for half in range(rows // 2):
                 flip = flip_banks.tile([P, 2, 2, P], F32, tag="flip")
                 for rr in range(2):
                     for u in range(2):
                         first = ((2 * half + rr) * 2 + u) * P
-                        nc.tensor.transpose(flip[:, rr, u, :], words[:, first : first + P], ident[:])
+                        nc.tensor.transpose(flip[:, rr, u, :], words_g[:, first : first + P], ident[:])
                 flips.append(flip)
-            for half, copy in enumerate((nc.scalar.copy, nc.scalar.copy if g < 2 else nc.vector.tensor_copy)):
+            for half, copy in zip(range(rows // 2), (nc.scalar.copy, nc.scalar.copy if g < 2 else nc.vector.tensor_copy)):
                 copy(
                     out=grouped_words[:, 2 * half : 2 * half + 2],
                     in_=flips[half][:].rearrange("p r u n -> p r n u"),
@@ -192,63 +212,87 @@ def tile_graphconvlayer_pb_kernel(tc, h, edge_features, Wu1_w, Wu1_b, Wu2_w, Wu2
             ef_grouped[g] = grouped
 
         def quantise_edges(g):
-            codes = stage.tile([P, GROUP], U32, align_bytes=64, tag="ef_codes")
-            scales = stage.tile([P, GROUP], U8, align_bytes=64, tag="ef_scales")
+            codes = stage.tile([P, GROUP_ROWS[g] * P], U32, align_bytes=64, tag="ef_codes")
+            scales = stage.tile([P, GROUP_ROWS[g] * P], U8, align_bytes=64, tag="ef_scales")
             nc.vector.quantize_mx(out=codes[:].bitcast(FP8X4), scales=scales[:], in_=ef_grouped[g][:])
             ef_q[g] = (codes, scales)
 
         def residual(g):
-            res_g = results.tile([P, ROWS, D], F32, tag="res")
+            rows = GROUP_ROWS[g]
+            mine = rows if g == 0 else rows // 2
+            res_g = results.tile([P, rows, D], F32, tag="res")
             nc.vector.tensor_tensor(
-                out=res_g[:, 0:VECTOR_ROWS],
-                in0=ef_sb[g][:].rearrange("p (r d) -> p r d", r=ROWS)[:, 0:VECTOR_ROWS],
-                in1=b2_all[:].unsqueeze(1).to_broadcast([P, VECTOR_ROWS, D]),
+                out=res_g[:, 0:mine],
+                in0=ef_sb[g][:].rearrange("p (r d) -> p r d", r=rows)[:, 0:mine],
+                in1=b2_all[:].unsqueeze(1).to_broadcast([P, mine, D]),
                 op=ADD,
             )
-            nc.vector.memset(res_g[:, VECTOR_ROWS, 0:8], 0.0)
-            for r in range(VECTOR_ROWS, ROWS):
+            if mine < rows:
+                nc.vector.memset(res_g[:, mine, 0:8], 0.0)
+            for r in range(mine, rows):
                 nc.gpsimd.tensor_tensor(out=res_g[:, r, :], in0=ef_sb[g][:, r * D : (r + 1) * D], in1=b2_all[:], op=ADD)
             res[g] = res_g
 
+        def first_layer_pass(g, t, blk, pre):
+            chunk = slice(t * P, (t + 1) * P)
+            edges = GROUP_ROWS[g] * P
+            first = FIRST_ROW[g] * P
+            if blk == 0:
+                moving = [(slice(0, edges), hi_codes[:, first : first + edges], hi_scales[:, first : first + edges])]
+            elif blk == 1:
+                moving = []
+                for pair in range(edges // PAIR):
+                    b = (first // PAIR + pair) // PAIRS_OF_GRAPH
+                    cols = slice(b * PAIR, (b + 1) * PAIR)
+                    moving.append((slice(pair * PAIR, (pair + 1) * PAIR), hj_codes[:, cols], hj_scales[:, cols]))
+            else:
+                moving = [(slice(0, edges), ef_q[g][0][:], ef_q[g][1][:])]
+            for cols, codes, scales in moving:
+                nc.tensor.matmul_mx(
+                    out=pre[:, cols],
+                    lhsT=w_codes[blk][:, chunk].bitcast(FP8X4),
+                    lhsT_scale=w_scales[blk][:, chunk],
+                    rhs=codes.bitcast(FP8X4),
+                    rhs_scale=scales,
+                    start=(blk == 0),
+                    stop=(blk == 2),
+                )
+
+        pre = {}
+
+        def first_layer_nodes(g, t):
+            pre_gt = mx_banks.tile([P, GROUP_ROWS[g] * P], F32, tag="mx")
+            first_layer_pass(g, t, 0, pre_gt)
+            first_layer_pass(g, t, 1, pre_gt)
+            pre[g, t] = pre_gt
+
         def first_layer(g):
-            b = g // 2
-            moving = (
-                (hi_codes[:, g * GROUP : (g + 1) * GROUP], hi_scales[:, g * GROUP : (g + 1) * GROUP]),
-                (hj_codes[:, b * GROUP : (b + 1) * GROUP], hj_scales[:, b * GROUP : (b + 1) * GROUP]),
-                (ef_q[g][0][:], ef_q[g][1][:]),
-            )
-            u_g = stage.tile([P, PACK, GROUP], BF16, tag="u_plain")
+            edges = GROUP_ROWS[g] * P
+            u_g = stage.tile([P, PACK, edges], BF16, tag="u_plain")
             for t in range(PACK):
-                chunk = slice(t * P, (t + 1) * P)
-                pre = mx_banks.tile([P, GROUP], F32, tag="mx")
-                for blk in range(3):
-                    nc.tensor.matmul_mx(
-                        out=pre[:],
-                        lhsT=w_codes[blk][:, chunk].bitcast(FP8X4),
-                        lhsT_scale=w_scales[blk][:, chunk],
-                        rhs=moving[blk][0].bitcast(FP8X4),
-                        rhs_scale=moving[blk][1],
-                        start=(blk == 0),
-                        stop=(blk == 2),
-                    )
-                nc.scalar.activation(out=u_g[:, t, :], in_=pre[:], func=GELU, bias=b1_col[:, t : t + 1], scale=1.0)
+                if (g, t) not in pre:
+                    first_layer_nodes(g, t)
+                first_layer_pass(g, t, 2, pre[g, t])
+                nc.scalar.activation(
+                    out=u_g[:, t, :], in_=pre[g, t][:], func=GELU, bias=b1_col[:, t : t + 1], scale=1.0
+                )
             u_plain[g] = u_g
 
         def regroup_u(g):
-            grouped = stage.tile([P, GROUP * PACK], BF16, align_bytes=64, tag="u_grouped")
+            grouped = stage.tile([P, GROUP_ROWS[g] * P * PACK], BF16, align_bytes=64, tag="u_grouped")
             dst, src = side_by_side_views(grouped[:], u_plain[g][:])
             nc.scalar.copy(out=dst, in_=src)
             u_grouped[g] = grouped
 
         def quantise_u(g):
-            codes = stage.tile([P, GROUP], U32, align_bytes=64, tag="u_codes")
-            scales = stage.tile([P, GROUP], U8, align_bytes=64, tag="u_scales")
+            codes = stage.tile([P, GROUP_ROWS[g] * P], U32, align_bytes=64, tag="u_codes")
+            scales = stage.tile([P, GROUP_ROWS[g] * P], U8, align_bytes=64, tag="u_scales")
             nc.vector.quantize_mx(out=codes[:].bitcast(FP8X4), scales=scales[:], in_=u_grouped[g][:])
             u_q[g] = (codes, scales)
 
         def second_layer(g):
             codes, scales = u_q[g]
-            for r in range(ROWS):
+            for r in range(GROUP_ROWS[g]):
                 edges = slice(r * P, (r + 1) * P)
                 prod = mx_banks.tile([P, D], F32, tag="mx")
                 nc.tensor.matmul_mx(
@@ -261,46 +305,55 @@ def tile_graphconvlayer_pb_kernel(tc, h, edge_features, Wu1_w, Wu1_b, Wu2_w, Wu2
                     stop=True,
                 )
                 nc.vector.tensor_tensor(out=res[g][:, r, :], in0=prod[:], in1=res[g][:, r, :], op=ADD)
-                nc.sync.dma_start(out=out_rows[g * GROUP + r * P : g * GROUP + (r + 1) * P, :], in_=res[g][:, r, :])
+                row = (FIRST_ROW[g] + r) * P
+                nc.sync.dma_start(out=out_rows[row : row + P, :], in_=res[g][:, r, :])
 
-        regroup_weights(0)
+        regroup_weights(0, VECTOR_COLUMNS)
         nc.vector.quantize_mx(out=four_codes[:].bitcast(FP8X4), scales=four_scales[:], in_=h_four[:])
-        regroup_weights(1)
-        spread_h(0, 1)
+        regroup_weights(1, VECTOR_COLUMNS)
+        spread_hi(0)
+        spread_hj(0, 1)
         quantise_weights(0)
-        regroup_weights(2)
-        quantise_weights(1)
         flip_edges(0)
         b1_wide = keep.tile([P, P], F32)
         nc.vector.tensor_copy(out=b1_wide[:], in_=b1_rows[:])
         b1_flip = mx_banks.tile([P, P], F32, tag="mx")
         nc.tensor.transpose(b1_flip[:], b1_wide[:], ident[:])
-        quantise_weights(2)
-        b1_col = keep.tile([P, PACK], F32)
-        nc.vector.tensor_copy(out=b1_col[:], in_=b1_flip[:, 0:PACK])
         b2_bank = mx_banks.tile([P, D], F32, tag="mx")
         nc.tensor.matmul(out=b2_bank[:], lhsT=ones[:], rhs=b2_row[:], start=True, stop=True)
-        b2_all = keep.tile([P, D], BF16)
-        nc.scalar.copy(out=b2_all[:], in_=b2_bank[:])
+        quantise_weights(1)
+        regroup_weights(2, VECTOR_COLUMNS)
+        flip_edges(1)
+        for t in range(PACK):
+            first_layer_nodes(0, t)
         quantise_edges(0)
+        b1_col = keep.tile([P, PACK], F32)
+        nc.vector.tensor_copy(out=b1_col[:], in_=b1_flip[:, 0:PACK])
+        quantise_weights(2)
+        b2_all = keep.tile([P, D], BF16)
 
         for r in range(GROUPS + 1):
-            if r + 1 < GROUPS:
+            if r + 1 < GROUPS and r > 0:
                 flip_edges(r + 1)
             if r >= 1:
                 quantise_u(r - 1)
-            if r + 1 < GROUPS:
+            if r + 1 < GROUPS and r > 0:
                 quantise_edges(r + 1)
-            if r == 0:
-                regroup_weights(3)
-            if 1 <= r < GROUPS:
+            if r >= 1 and r < GROUPS:
                 residual(r)
             if r < GROUPS:
                 first_layer(r)
             if r == 0:
+                quantise_edges(1)
+                nc.scalar.copy(out=b2_all[:], in_=b2_bank[:])
+                spread_hi(1)
+                regroup_weights(3, D)
+                spread_hi(2)
+                spread_hj(1, GRAPHS - 1)
                 quantise_weights(3)
-                spread_h(1, GRAPHS - 1)
                 residual(0)
+            if r >= 1 and r + 2 < GROUPS:
+                spread_hi(r + 2)
             if r >= 1:
                 second_layer(r - 1)
             if r < GROUPS:

@@ -103,29 +103,29 @@ def tile_graphconvlayer_pb_kernel(tc, h, edge_features, Wu1_w, Wu1_b, Wu2_w, Wu2
             src = planes.rearrange("p t (c i) -> p c t i", i=RUN)
             return dst, src
 
-        once_codes = keep.tile([P, GRAPHS * NODES], U32, align_bytes=64)
-        once_scales = keep.tile([P, GRAPHS * NODES], U8, align_bytes=64)
-        four_codes = keep.tile([P, GRAPHS * NODES * WORD_BYTES], U32, align_bytes=64)
-        four_scales = keep.tile([P, GRAPHS * NODES * WORD_BYTES], U8, align_bytes=64)
+        once_codes = keep.tile([P, GRAPHS * NODES], U32, align_bytes=256)
+        once_scales = keep.tile([P, GRAPHS * NODES], U8, align_bytes=256)
+        four_codes = keep.tile([P, GRAPHS * NODES * WORD_BYTES], U32, align_bytes=256)
+        four_scales = keep.tile([P, GRAPHS * NODES * WORD_BYTES], U8, align_bytes=256)
         nc.vector.memset(once_scales[:].bitcast(I32), 0)
         nc.vector.memset(four_scales[:].bitcast(I32), 0)
         h_flip = mx_banks.tile([P, 2, P], F32, tag="mx")
         for u in range(2):
             nc.tensor.transpose(h_flip[:, u, :], h_sb[:].bitcast(F32)[:, u * P : (u + 1) * P], ident[:])
         h_flip_nu = h_flip[:].rearrange("p u n -> p n u")
-        h_once = keep.tile([P, GRAPHS * NODES * PACK], BF16, align_bytes=64)
+        h_once = keep.tile([P, GRAPHS * NODES * PACK], BF16, align_bytes=256)
         nc.vector.tensor_copy(out=h_once[:].bitcast(F32).rearrange("p (n u) -> p n u", u=2), in_=h_flip_nu)
-        h_four = keep.tile([P, GRAPHS * NODES * WORD_BYTES * PACK], BF16, align_bytes=64)
+        h_four = keep.tile([P, GRAPHS * NODES * WORD_BYTES * PACK], BF16, align_bytes=256)
         nc.scalar.copy(
             out=h_four[:].bitcast(F32).rearrange("p (n w u) -> p n w u", w=WORD_BYTES, u=2),
             in_=h_flip_nu.unsqueeze(2).to_broadcast([P, GRAPHS * NODES, WORD_BYTES, 2]),
         )
         nc.vector.quantize_mx(out=once_codes[:].bitcast(FP8X4), scales=once_scales[:], in_=h_once[:])
 
-        hi_codes = keep.tile([P, EDGES], U32, align_bytes=64)
-        hi_scales = keep.tile([P, EDGES], U8, align_bytes=64)
-        hj_codes = keep.tile([P, GRAPHS * PAIR], U32, align_bytes=64)
-        hj_scales = keep.tile([P, GRAPHS * PAIR], U8, align_bytes=64)
+        hi_codes = keep.tile([P, EDGES], U32, align_bytes=256)
+        hi_scales = keep.tile([P, EDGES], U8, align_bytes=256)
+        hj_codes = keep.tile([P, GRAPHS * PAIR], U32, align_bytes=256)
+        hj_scales = keep.tile([P, GRAPHS * PAIR], U8, align_bytes=256)
 
         words = NODES // WORD_BYTES
         nodes_of_row = P // NODES
@@ -169,7 +169,7 @@ def tile_graphconvlayer_pb_kernel(tc, h, edge_features, Wu1_w, Wu1_b, Wu2_w, Wu2
         w_scales = {}
 
         def regroup_weights(blk, vector_columns):
-            grouped = keep.tile([P, D * PACK], BF16, align_bytes=64, name="w_grouped%d" % blk)
+            grouped = keep.tile([P, D * PACK], BF16, align_bytes=256, name="w_grouped%d" % blk)
             dst, src = side_by_side_views(grouped[:], w_raw[blk][:])
             cut = vector_columns // RUN
             nc.vector.tensor_copy(out=dst[:, 0:cut], in_=src[:, 0:cut])
@@ -178,8 +178,8 @@ def tile_graphconvlayer_pb_kernel(tc, h, edge_features, Wu1_w, Wu1_b, Wu2_w, Wu2
             w_grouped[blk] = grouped
 
         def quantise_weights(blk):
-            codes = keep.tile([P, D], U32, align_bytes=64, name="w_codes%d" % blk)
-            scales = keep.tile([P, D], U8, align_bytes=64, name="w_scales%d" % blk)
+            codes = keep.tile([P, D], U32, align_bytes=256, name="w_codes%d" % blk)
+            scales = keep.tile([P, D], U8, align_bytes=256, name="w_scales%d" % blk)
             nc.vector.quantize_mx(out=codes[:].bitcast(FP8X4), scales=scales[:], in_=w_grouped[blk][:])
             w_codes[blk] = codes
             w_scales[blk] = scales
@@ -194,7 +194,7 @@ def tile_graphconvlayer_pb_kernel(tc, h, edge_features, Wu1_w, Wu1_b, Wu2_w, Wu2
         def flip_edges(g):
             rows = GROUP_ROWS[g]
             words_g = ef_sb[g][:].bitcast(F32)
-            grouped = stage.tile([P, rows * P * PACK], BF16, align_bytes=64, tag="ef_grouped")
+            grouped = stage.tile([P, rows * P * PACK], BF16, align_bytes=256, tag="ef_grouped")
             grouped_words = grouped[:].bitcast(F32).rearrange("p (r n u) -> p r n u", r=rows, u=2)
             flips = []
             for half in range(rows // 2):
@@ -212,8 +212,8 @@ def tile_graphconvlayer_pb_kernel(tc, h, edge_features, Wu1_w, Wu1_b, Wu2_w, Wu2
             ef_grouped[g] = grouped
 
         def quantise_edges(g):
-            codes = stage.tile([P, GROUP_ROWS[g] * P], U32, align_bytes=64, tag="ef_codes")
-            scales = stage.tile([P, GROUP_ROWS[g] * P], U8, align_bytes=64, tag="ef_scales")
+            codes = stage.tile([P, GROUP_ROWS[g] * P], U32, align_bytes=256, tag="ef_codes")
+            scales = stage.tile([P, GROUP_ROWS[g] * P], U8, align_bytes=256, tag="ef_scales")
             nc.vector.quantize_mx(out=codes[:].bitcast(FP8X4), scales=scales[:], in_=ef_grouped[g][:])
             ef_q[g] = (codes, scales)
 
@@ -279,14 +279,14 @@ def tile_graphconvlayer_pb_kernel(tc, h, edge_features, Wu1_w, Wu1_b, Wu2_w, Wu2
             u_plain[g] = u_g
 
         def regroup_u(g):
-            grouped = stage.tile([P, GROUP_ROWS[g] * P * PACK], BF16, align_bytes=64, tag="u_grouped")
+            grouped = stage.tile([P, GROUP_ROWS[g] * P * PACK], BF16, align_bytes=256, tag="u_grouped")
             dst, src = side_by_side_views(grouped[:], u_plain[g][:])
             nc.scalar.copy(out=dst, in_=src)
             u_grouped[g] = grouped
 
         def quantise_u(g):
-            codes = stage.tile([P, GROUP_ROWS[g] * P], U32, align_bytes=64, tag="u_codes")
-            scales = stage.tile([P, GROUP_ROWS[g] * P], U8, align_bytes=64, tag="u_scales")
+            codes = stage.tile([P, GROUP_ROWS[g] * P], U32, align_bytes=256, tag="u_codes")
+            scales = stage.tile([P, GROUP_ROWS[g] * P], U8, align_bytes=256, tag="u_scales")
             nc.vector.quantize_mx(out=codes[:].bitcast(FP8X4), scales=scales[:], in_=u_grouped[g][:])
             u_q[g] = (codes, scales)
 
@@ -295,6 +295,8 @@ def tile_graphconvlayer_pb_kernel(tc, h, edge_features, Wu1_w, Wu1_b, Wu2_w, Wu2
             for r in range(GROUP_ROWS[g]):
                 edges = slice(r * P, (r + 1) * P)
                 prod = mx_banks.tile([P, D], F32, tag="mx")
+                if g == GROUPS - 2 and r == 2:
+                    quantise_u(GROUPS - 1)
                 nc.tensor.matmul_mx(
                     out=prod[:],
                     lhsT=codes[:, edges].bitcast(FP8X4),
@@ -335,7 +337,7 @@ def tile_graphconvlayer_pb_kernel(tc, h, edge_features, Wu1_w, Wu1_b, Wu2_w, Wu2
         for r in range(GROUPS + 1):
             if r + 1 < GROUPS and r > 0:
                 flip_edges(r + 1)
-            if r >= 1:
+            if 1 <= r < GROUPS:
                 quantise_u(r - 1)
             if r + 1 < GROUPS and r > 0:
                 quantise_edges(r + 1)
@@ -354,7 +356,9 @@ def tile_graphconvlayer_pb_kernel(tc, h, edge_features, Wu1_w, Wu1_b, Wu2_w, Wu2
                 residual(0)
             if r >= 1 and r + 2 < GROUPS:
                 spread_hi(r + 2)
+            if r == GROUPS - 1:
+                regroup_u(r)
             if r >= 1:
                 second_layer(r - 1)
-            if r < GROUPS:
+            if r < GROUPS - 1:
                 regroup_u(r)

@@ -21,13 +21,11 @@ EDGES = GRAPHS * NODES * NODES
 GROUP_ROWS = [2, 4, 4, 4, 4, 4, 4, 4, 2]
 GROUPS = len(GROUP_ROWS)
 FIRST_ROW = [sum(GROUP_ROWS[:g]) for g in range(GROUPS)]
-PAIR = 2 * P
-I_OF_PAIR = PAIR // NODES
-PAIRS_OF_GRAPH = NODES * NODES // PAIR
+GROUP = max(GROUP_ROWS) * P
 WORD_BYTES = 4
 RUN = 4
 
-VECTOR_COLUMNS = 272
+VECTOR_COLUMNS = 240
 
 
 FLOPS = 2 * D * D * (2 * GRAPHS * NODES + 2 * EDGES)
@@ -36,8 +34,8 @@ FLOPS = 2 * D * D * (2 * GRAPHS * NODES + 2 * EDGES)
 def tile_graphconvlayer_pb_kernel(tc, h, edge_features, Wu1_w, Wu1_b, Wu2_w, Wu2_b, out):
     nc = tc.nc
     h_rows = h.rearrange("b n d -> (b n) d")
-    ef_rows = edge_features.rearrange("b i j d -> (b i j) d")
-    out_rows = out.rearrange("b i j d -> (b i j) d")
+    ef_rows = edge_features.rearrange("b i j d -> (b i) j d")
+    out_rows = out.rearrange("b i j d -> (b i) j d")
 
     with ExitStack() as ctx:
         ctx.enter_context(tc.manual_schedule())
@@ -65,11 +63,10 @@ def tile_graphconvlayer_pb_kernel(tc, h, edge_features, Wu1_w, Wu1_b, Wu2_w, Wu2
 
         def load_edges(g):
             rows = GROUP_ROWS[g]
-            first = FIRST_ROW[g] * P
             ef_g = keep.tile([P, rows * D], BF16, name="ef%d" % g)
             nc.sync.dma_start(
                 out=ef_g[:].rearrange("p (r d) -> p r d", r=rows),
-                in_=ef_rows[first : first + rows * P, :].rearrange("(r p) d -> p r d", p=P),
+                in_=ef_rows[:, FIRST_ROW[g] : FIRST_ROW[g] + rows, :],
             )
             ef_sb[g] = ef_g
 
@@ -105,64 +102,48 @@ def tile_graphconvlayer_pb_kernel(tc, h, edge_features, Wu1_w, Wu1_b, Wu2_w, Wu2
 
         once_codes = keep.tile([P, GRAPHS * NODES], U32, align_bytes=256)
         once_scales = keep.tile([P, GRAPHS * NODES], U8, align_bytes=256)
-        four_codes = keep.tile([P, GRAPHS * NODES * WORD_BYTES], U32, align_bytes=256)
         four_scales = keep.tile([P, GRAPHS * NODES * WORD_BYTES], U8, align_bytes=256)
         nc.vector.memset(once_scales[:].bitcast(I32), 0)
-        nc.vector.memset(four_scales[:].bitcast(I32), 0)
         h_flip = mx_banks.tile([P, 2, P], F32, tag="mx")
         for u in range(2):
             nc.tensor.transpose(h_flip[:, u, :], h_sb[:].bitcast(F32)[:, u * P : (u + 1) * P], ident[:])
         h_flip_nu = h_flip[:].rearrange("p u n -> p n u")
         h_once = keep.tile([P, GRAPHS * NODES * PACK], BF16, align_bytes=256)
         nc.vector.tensor_copy(out=h_once[:].bitcast(F32).rearrange("p (n u) -> p n u", u=2), in_=h_flip_nu)
-        h_four = keep.tile([P, GRAPHS * NODES * WORD_BYTES * PACK], BF16, align_bytes=256)
-        nc.scalar.copy(
-            out=h_four[:].bitcast(F32).rearrange("p (n w u) -> p n w u", w=WORD_BYTES, u=2),
-            in_=h_flip_nu.unsqueeze(2).to_broadcast([P, GRAPHS * NODES, WORD_BYTES, 2]),
-        )
         nc.vector.quantize_mx(out=once_codes[:].bitcast(FP8X4), scales=once_scales[:], in_=h_once[:])
 
-        hi_codes = keep.tile([P, EDGES], U32, align_bytes=256)
-        hi_scales = keep.tile([P, EDGES], U8, align_bytes=256)
-        hj_codes = keep.tile([P, GRAPHS * PAIR], U32, align_bytes=256)
-        hj_scales = keep.tile([P, GRAPHS * PAIR], U8, align_bytes=256)
+        hi_codes = keep.tile([P, GROUP], U32, align_bytes=256)
+        hi_scales = keep.tile([P, GROUP], U8, align_bytes=256)
+        hj_codes = keep.tile([P, EDGES], U32, align_bytes=256)
+        hj_scales = keep.tile([P, EDGES], U8, align_bytes=256)
 
-        words = NODES // WORD_BYTES
-        nodes_of_row = P // NODES
-
-        def spread_hi(g):
-            nodes = slice(FIRST_ROW[g] * nodes_of_row, (FIRST_ROW[g] + GROUP_ROWS[g]) * nodes_of_row)
-            count = GROUP_ROWS[g] * nodes_of_row
+        def repeat_scales(w):
             nc.vector.tensor_copy(
-                out=hi_codes[:].bitcast(I32).rearrange("p (n j) -> p n j", j=NODES)[:, nodes, :],
-                in_=four_codes[:]
-                .bitcast(I32)
-                .rearrange("p (n w) -> p n w", w=WORD_BYTES)[:, nodes, 0:1]
-                .to_broadcast([P, count, NODES]),
-            )
-            nc.vector.tensor_copy(
-                out=hi_scales[:].bitcast(I32).rearrange("p (n w) -> p n w", w=words)[:, nodes, :],
-                in_=four_scales[:].bitcast(I32)[:, nodes].unsqueeze(2).to_broadcast([P, count, words]),
+                out=four_scales[:].rearrange("p (n w) -> p n w", w=WORD_BYTES)[:, :, w], in_=once_scales[:]
             )
 
-        def spread_hj(first, count):
-            graphs = slice(first, first + count)
-            nc.vector.tensor_copy(
-                out=hj_codes[:].bitcast(I32).rearrange("p (b i j) -> p b i j", i=I_OF_PAIR, j=NODES)[:, graphs],
-                in_=once_codes[:]
-                .bitcast(I32)
-                .rearrange("p (b j) -> p b j", j=NODES)[:, graphs]
-                .unsqueeze(2)
-                .to_broadcast([P, count, I_OF_PAIR, NODES]),
-            )
-            nc.vector.tensor_copy(
-                out=hj_scales[:].bitcast(I32).rearrange("p (b i w) -> p b i w", i=I_OF_PAIR, w=words)[:, graphs],
-                in_=once_scales[:]
-                .bitcast(I32)
-                .rearrange("p (b w) -> p b w", w=words)[:, graphs]
-                .unsqueeze(2)
-                .to_broadcast([P, count, I_OF_PAIR, words]),
-            )
+        def spread_hi():
+            for spread, once in ((hi_codes, once_codes), (hi_scales, once_scales)):
+                words = once[:].bitcast(I32)
+                nc.vector.tensor_copy(
+                    out=spread[:].bitcast(I32).rearrange("p (r n) -> p r n", r=GROUP // P),
+                    in_=words.unsqueeze(1).to_broadcast([P, GROUP // P, words.shape[1]]),
+                )
+
+        def spread_hj(g):
+            rows = slice(FIRST_ROW[g], FIRST_ROW[g] + GROUP_ROWS[g])
+            for spread, once, count in (
+                (hj_codes, once_codes, NODES),
+                (hj_scales, four_scales, NODES // WORD_BYTES),
+            ):
+                nc.vector.tensor_copy(
+                    out=spread[:].bitcast(I32).rearrange("p (j b i) -> p j b i", b=GRAPHS, i=count)[:, rows],
+                    in_=once[:]
+                    .bitcast(I32)
+                    .rearrange("p (b j) -> p j b", b=GRAPHS)[:, rows]
+                    .unsqueeze(3)
+                    .to_broadcast([P, GROUP_ROWS[g], GRAPHS, count]),
+                )
 
         w_grouped = {}
         w_codes = {}
@@ -204,7 +185,7 @@ def tile_graphconvlayer_pb_kernel(tc, h, edge_features, Wu1_w, Wu1_b, Wu2_w, Wu2
                         first = ((2 * half + rr) * 2 + u) * P
                         nc.tensor.transpose(flip[:, rr, u, :], words_g[:, first : first + P], ident[:])
                 flips.append(flip)
-            for half, copy in zip(range(rows // 2), (nc.scalar.copy, nc.scalar.copy if g < 2 else nc.vector.tensor_copy)):
+            for half, copy in zip(range(rows // 2), (nc.scalar.copy, nc.scalar.copy if g < 2 or g % 2 == 0 else nc.vector.tensor_copy)):
                 copy(
                     out=grouped_words[:, 2 * half : 2 * half + 2],
                     in_=flips[half][:].rearrange("p r u n -> p r n u"),
@@ -215,7 +196,7 @@ def tile_graphconvlayer_pb_kernel(tc, h, edge_features, Wu1_w, Wu1_b, Wu2_w, Wu2
             codes = stage.tile([P, GROUP_ROWS[g] * P], U32, align_bytes=256, tag="ef_codes")
             scales = stage.tile([P, GROUP_ROWS[g] * P], U8, align_bytes=256, tag="ef_scales")
             nc.vector.quantize_mx(out=codes[:].bitcast(FP8X4), scales=scales[:], in_=ef_grouped[g][:])
-            ef_q[g] = (codes, scales)
+            ef_q[g] = (codes[:], scales[:])
 
         def residual(g):
             rows = GROUP_ROWS[g]
@@ -233,30 +214,24 @@ def tile_graphconvlayer_pb_kernel(tc, h, edge_features, Wu1_w, Wu1_b, Wu2_w, Wu2
                 nc.gpsimd.tensor_tensor(out=res_g[:, r, :], in0=ef_sb[g][:, r * D : (r + 1) * D], in1=b2_all[:], op=ADD)
             res[g] = res_g
 
-        def first_layer_pass(g, t, blk, pre):
+        def first_layer_pass(g, t, blk, pre_gt):
             chunk = slice(t * P, (t + 1) * P)
             edges = GROUP_ROWS[g] * P
             first = FIRST_ROW[g] * P
-            if blk == 0:
-                moving = [(slice(0, edges), hi_codes[:, first : first + edges], hi_scales[:, first : first + edges])]
-            elif blk == 1:
-                moving = []
-                for pair in range(edges // PAIR):
-                    b = (first // PAIR + pair) // PAIRS_OF_GRAPH
-                    cols = slice(b * PAIR, (b + 1) * PAIR)
-                    moving.append((slice(pair * PAIR, (pair + 1) * PAIR), hj_codes[:, cols], hj_scales[:, cols]))
-            else:
-                moving = [(slice(0, edges), ef_q[g][0][:], ef_q[g][1][:])]
-            for cols, codes, scales in moving:
-                nc.tensor.matmul_mx(
-                    out=pre[:, cols],
-                    lhsT=w_codes[blk][:, chunk].bitcast(FP8X4),
-                    lhsT_scale=w_scales[blk][:, chunk],
-                    rhs=codes.bitcast(FP8X4),
-                    rhs_scale=scales,
-                    start=(blk == 0),
-                    stop=(blk == 2),
-                )
+            moving, moving_scales = (
+                (hi_codes[:, 0:edges], hi_scales[:, 0:edges]),
+                (hj_codes[:, first : first + edges], hj_scales[:, first : first + edges]),
+                ef_q.get(g),
+            )[blk]
+            nc.tensor.matmul_mx(
+                out=pre_gt[:],
+                lhsT=w_codes[blk][:, chunk].bitcast(FP8X4),
+                lhsT_scale=w_scales[blk][:, chunk],
+                rhs=moving.bitcast(FP8X4),
+                rhs_scale=moving_scales,
+                start=(blk == 0),
+                stop=(blk == 2),
+            )
 
         pre = {}
 
@@ -307,15 +282,16 @@ def tile_graphconvlayer_pb_kernel(tc, h, edge_features, Wu1_w, Wu1_b, Wu2_w, Wu2
                     stop=True,
                 )
                 nc.vector.tensor_tensor(out=res[g][:, r, :], in0=prod[:], in1=res[g][:, r, :], op=ADD)
-                row = (FIRST_ROW[g] + r) * P
-                nc.sync.dma_start(out=out_rows[row : row + P, :], in_=res[g][:, r, :])
+                nc.sync.dma_start(out=out_rows[:, FIRST_ROW[g] + r, :], in_=res[g][:, r, :])
 
         regroup_weights(0, VECTOR_COLUMNS)
-        nc.vector.quantize_mx(out=four_codes[:].bitcast(FP8X4), scales=four_scales[:], in_=h_four[:])
+        repeat_scales(0)
         regroup_weights(1, VECTOR_COLUMNS)
-        spread_hi(0)
-        spread_hj(0, 1)
+        repeat_scales(1)
+        spread_hi()
+        repeat_scales(2)
         quantise_weights(0)
+        repeat_scales(3)
         flip_edges(0)
         b1_wide = keep.tile([P, P], F32)
         nc.vector.tensor_copy(out=b1_wide[:], in_=b1_rows[:])
@@ -324,6 +300,7 @@ def tile_graphconvlayer_pb_kernel(tc, h, edge_features, Wu1_w, Wu1_b, Wu2_w, Wu2
         b2_bank = mx_banks.tile([P, D], F32, tag="mx")
         nc.tensor.matmul(out=b2_bank[:], lhsT=ones[:], rhs=b2_row[:], start=True, stop=True)
         quantise_weights(1)
+        spread_hj(0)
         regroup_weights(2, VECTOR_COLUMNS)
         flip_edges(1)
         for t in range(PACK):
@@ -348,14 +325,13 @@ def tile_graphconvlayer_pb_kernel(tc, h, edge_features, Wu1_w, Wu1_b, Wu2_w, Wu2
             if r == 0:
                 quantise_edges(1)
                 nc.scalar.copy(out=b2_all[:], in_=b2_bank[:])
-                spread_hi(1)
+                spread_hj(1)
                 regroup_weights(3, D)
-                spread_hi(2)
-                spread_hj(1, GRAPHS - 1)
+                spread_hj(2)
                 quantise_weights(3)
                 residual(0)
             if r >= 1 and r + 2 < GROUPS:
-                spread_hi(r + 2)
+                spread_hj(r + 2)
             if r == GROUPS - 1:
                 regroup_u(r)
             if r >= 1:

@@ -25,7 +25,7 @@ GROUP = max(GROUP_ROWS) * P
 WORD_BYTES = 4
 RUN = 4
 
-VECTOR_COLUMNS = 240
+VECTOR_COLUMNS = 208
 
 
 FLOPS = 2 * D * D * (2 * GRAPHS * NODES + 2 * EDGES)
@@ -185,7 +185,7 @@ def tile_graphconvlayer_pb_kernel(tc, h, edge_features, Wu1_w, Wu1_b, Wu2_w, Wu2
                         first = ((2 * half + rr) * 2 + u) * P
                         nc.tensor.transpose(flip[:, rr, u, :], words_g[:, first : first + P], ident[:])
                 flips.append(flip)
-            for half, copy in zip(range(rows // 2), (nc.scalar.copy, nc.scalar.copy if g < 2 or g % 2 == 0 else nc.vector.tensor_copy)):
+            for half, copy in zip(range(rows // 2), (nc.vector.tensor_copy if g == 3 else nc.scalar.copy, nc.scalar.copy if g < 2 or g % 2 == 0 else nc.vector.tensor_copy)):
                 copy(
                     out=grouped_words[:, 2 * half : 2 * half + 2],
                     in_=flips[half][:].rearrange("p r u n -> p r n u"),

from contextlib import ExitStack

import concourse.masks as masks
import concourse.mybir as mybir

F32 = mybir.dt.float32
BF16 = mybir.dt.bfloat16
I32 = mybir.dt.int32
U32 = mybir.dt.uint32
U8 = mybir.dt.uint8
FP8X4 = mybir.dt.float8_e4m3fn_x4
ADD = mybir.AluOpType.add
GELU = mybir.ActivationFunctionType.Gelu

P = 128
PACK = 4
D = P * PACK
GRAPHS = 4
NODES = 32
EDGES = GRAPHS * NODES * NODES
GROUP_ROWS = [2, 4, 4, 4, 4, 4, 4, 4, 2]
GROUPS = len(GROUP_ROWS)
FIRST_ROW = [sum(GROUP_ROWS[:g]) for g in range(GROUPS)]
GROUP = max(GROUP_ROWS) * P
WORD_BYTES = 4
RUN = 4

VECTOR_COLUMNS = 208


FLOPS = 2 * D * D * (2 * GRAPHS * NODES + 2 * EDGES)


def tile_graphconvlayer_pb_kernel(tc, h, edge_features, Wu1_w, Wu1_b, Wu2_w, Wu2_b, out):
    nc = tc.nc
    h_rows = h.rearrange("b n d -> (b n) d")
    ef_rows = edge_features.rearrange("b i j d -> (b i) j d")
    out_rows = out.rearrange("b i j d -> (b i) j d")

    with ExitStack() as ctx:
        ctx.enter_context(tc.manual_schedule())
        keep = ctx.enter_context(tc.tile_pool(name="keep", bufs=1))
        stage = ctx.enter_context(tc.tile_pool(name="stage", bufs=2))
        results = ctx.enter_context(tc.tile_pool(name="results", bufs=4))
        flip_banks = ctx.enter_context(tc.psum_pool(name="flip_banks", bufs=2))
        mx_banks = ctx.enter_context(tc.psum_pool(name="mx_banks", bufs=6))

        h_sb = keep.tile([P, D], BF16)
        nc.sync.dma_start(out=h_sb[:], in_=h_rows)
        w_raw = {}
        ef_sb = {}

        def load_weights(blk):
            raw = keep.tile([P, PACK, D], BF16, name="w_raw%d" % blk)
            if blk == 3:
                nc.sync.dma_start(out=raw[:], in_=Wu2_w.rearrange("(t p) c -> p t c", p=P))
            else:
                nc.sync.dma_start(
                    out=raw[:].rearrange("p (u e) c -> p u e c", u=2),
                    in_=Wu1_w[blk * D : (blk + 1) * D, :].rearrange("(u p e) c -> p u e c", u=2, e=2),
                )
            w_raw[blk] = raw

        def load_edges(g):
            rows = GROUP_ROWS[g]
            ef_g = keep.tile([P, rows * D], BF16, name="ef%d" % g)
            nc.sync.dma_start(
                out=ef_g[:].rearrange("p (r d) -> p r d", r=rows),
                in_=ef_rows[:, FIRST_ROW[g] : FIRST_ROW[g] + rows, :],
            )
            ef_sb[g] = ef_g

        load_weights(0)
        load_weights(1)
        load_edges(0)
        load_weights(2)
        load_edges(1)
        load_weights(3)
        for g in range(2, GROUPS):
            load_edges(g)

        b1_rows = keep.tile([P, P], BF16)
        nc.vector.memset(b1_rows[:], 0.0)
        nc.scalar.dma_start(out=b1_rows[0:PACK, :], in_=Wu1_b.rearrange("(t p) -> t p", p=P))
        b2_row = keep.tile([P, D], BF16)
        nc.vector.memset(b2_row[:], 0.0)
        nc.scalar.dma_start(out=b2_row[0:1, :], in_=Wu2_b.rearrange("(o d) -> o d", o=1))
        ones = keep.tile([P, P], BF16)
        nc.vector.memset(ones[:], 1.0)

        warm = keep.tile([P, 1], F32)
        nc.vector.memset(warm[:], 0.0)
        nc.scalar.activation(out=warm[:], in_=warm[:], func=GELU)

        ident = keep.tile([P, P], F32)
        masks.make_identity(nc, ident[:])

        def side_by_side_views(grouped, planes):
            dst = grouped.rearrange("p (c i t) -> p c t i", i=RUN, t=PACK)
            src = planes.rearrange("p t (c i) -> p c t i", i=RUN)
            return dst, src

        once_codes = keep.tile([P, GRAPHS * NODES], U32, align_bytes=256)
        once_scales = keep.tile([P, GRAPHS * NODES], U8, align_bytes=256)
        four_scales = keep.tile([P, GRAPHS * NODES * WORD_BYTES], U8, align_bytes=256)
        nc.vector.memset(once_scales[:].bitcast(I32), 0)
        h_flip = mx_banks.tile([P, 2, P], F32, tag="mx")
        for u in range(2):
            nc.tensor.transpose(h_flip[:, u, :], h_sb[:].bitcast(F32)[:, u * P : (u + 1) * P], ident[:])
        h_flip_nu = h_flip[:].rearrange("p u n -> p n u")
        h_once = keep.tile([P, GRAPHS * NODES * PACK], BF16, align_bytes=256)
        nc.vector.tensor_copy(out=h_once[:].bitcast(F32).rearrange("p (n u) -> p n u", u=2), in_=h_flip_nu)
        nc.vector.quantize_mx(out=once_codes[:].bitcast(FP8X4), scales=once_scales[:], in_=h_once[:])

        hi_codes = keep.tile([P, GROUP], U32, align_bytes=256)
        hi_scales = keep.tile([P, GROUP], U8, align_bytes=256)
        hj_codes = keep.tile([P, EDGES], U32, align_bytes=256)
        hj_scales = keep.tile([P, EDGES], U8, align_bytes=256)

        def repeat_scales(w):
            nc.vector.tensor_copy(
                out=four_scales[:].rearrange("p (n w) -> p n w", w=WORD_BYTES)[:, :, w], in_=once_scales[:]
            )

        def spread_hi():
            for spread, once in ((hi_codes, once_codes), (hi_scales, once_scales)):
                words = once[:].bitcast(I32)
                nc.vector.tensor_copy(
                    out=spread[:].bitcast(I32).rearrange("p (r n) -> p r n", r=GROUP // P),
                    in_=words.unsqueeze(1).to_broadcast([P, GROUP // P, words.shape[1]]),
                )

        def spread_hj(g):
            rows = slice(FIRST_ROW[g], FIRST_ROW[g] + GROUP_ROWS[g])
            for spread, once, count in (
                (hj_codes, once_codes, NODES),
                (hj_scales, four_scales, NODES // WORD_BYTES),
            ):
                nc.vector.tensor_copy(
                    out=spread[:].bitcast(I32).rearrange("p (j b i) -> p j b i", b=GRAPHS, i=count)[:, rows],
                    in_=once[:]
                    .bitcast(I32)
                    .rearrange("p (b j) -> p j b", b=GRAPHS)[:, rows]
                    .unsqueeze(3)
                    .to_broadcast([P, GROUP_ROWS[g], GRAPHS, count]),
                )

        w_grouped = {}
        w_codes = {}
        w_scales = {}

        def regroup_weights(blk, vector_columns):
            grouped = keep.tile([P, D * PACK], BF16, align_bytes=256, name="w_grouped%d" % blk)
            dst, src = side_by_side_views(grouped[:], w_raw[blk][:])
            cut = vector_columns // RUN
            nc.vector.tensor_copy(out=dst[:, 0:cut], in_=src[:, 0:cut])
            if vector_columns < D:
                nc.scalar.copy(out=dst[:, cut:], in_=src[:, cut:])
            w_grouped[blk] = grouped

        def quantise_weights(blk):
            codes = keep.tile([P, D], U32, align_bytes=256, name="w_codes%d" % blk)
            scales = keep.tile([P, D], U8, align_bytes=256, name="w_scales%d" % blk)
            nc.vector.quantize_mx(out=codes[:].bitcast(FP8X4), scales=scales[:], in_=w_grouped[blk][:])
            w_codes[blk] = codes
            w_scales[blk] = scales

        ef_grouped = {}
        ef_q = {}
        u_plain = {}
        u_grouped = {}
        u_q = {}
        res = {}

        def flip_edges(g):
            rows = GROUP_ROWS[g]
            words_g = ef_sb[g][:].bitcast(F32)
            grouped = stage.tile([P, rows * P * PACK], BF16, align_bytes=256, tag="ef_grouped")
            grouped_words = grouped[:].bitcast(F32).rearrange("p (r n u) -> p r n u", r=rows, u=2)
            flips = []
            for half in range(rows // 2):
                flip = flip_banks.tile([P, 2, 2, P], F32, tag="flip")
                for rr in range(2):
                    for u in range(2):
                        first = ((2 * half + rr) * 2 + u) * P
                        nc.tensor.transpose(flip[:, rr, u, :], words_g[:, first : first + P], ident[:])
                flips.append(flip)
            for half, copy in zip(range(rows // 2), (nc.vector.tensor_copy if g == 3 else nc.scalar.copy, nc.scalar.copy if g < 2 or g % 2 == 0 else nc.vector.tensor_copy)):
                copy(
                    out=grouped_words[:, 2 * half : 2 * half + 2],
                    in_=flips[half][:].rearrange("p r u n -> p r n u"),
                )
            ef_grouped[g] = grouped

        def quantise_edges(g):
            codes = stage.tile([P, GROUP_ROWS[g] * P], U32, align_bytes=256, tag="ef_codes")
            scales = stage.tile([P, GROUP_ROWS[g] * P], U8, align_bytes=256, tag="ef_scales")
            nc.vector.quantize_mx(out=codes[:].bitcast(FP8X4), scales=scales[:], in_=ef_grouped[g][:])
            ef_q[g] = (codes[:], scales[:])

        def residual(g):
            rows = GROUP_ROWS[g]
            mine = rows if g == 0 else rows // 2
            res_g = results.tile([P, rows, D], F32, tag="res")
            nc.vector.tensor_tensor(
                out=res_g[:, 0:mine],
                in0=ef_sb[g][:].rearrange("p (r d) -> p r d", r=rows)[:, 0:mine],
                in1=b2_all[:].unsqueeze(1).to_broadcast([P, mine, D]),
                op=ADD,
            )
            if mine < rows:
                nc.vector.memset(res_g[:, mine, 0:8], 0.0)
            for r in range(mine, rows):
                nc.gpsimd.tensor_tensor(out=res_g[:, r, :], in0=ef_sb[g][:, r * D : (r + 1) * D], in1=b2_all[:], op=ADD)
            res[g] = res_g

        def first_layer_pass(g, t, blk, pre_gt):
            chunk = slice(t * P, (t + 1) * P)
            edges = GROUP_ROWS[g] * P
            first = FIRST_ROW[g] * P
            moving, moving_scales = (
                (hi_codes[:, 0:edges], hi_scales[:, 0:edges]),
                (hj_codes[:, first : first + edges], hj_scales[:, first : first + edges]),
                ef_q.get(g),
            )[blk]
            nc.tensor.matmul_mx(
                out=pre_gt[:],
                lhsT=w_codes[blk][:, chunk].bitcast(FP8X4),
                lhsT_scale=w_scales[blk][:, chunk],
                rhs=moving.bitcast(FP8X4),
                rhs_scale=moving_scales,
                start=(blk == 0),
                stop=(blk == 2),
            )

        pre = {}

        def first_layer_nodes(g, t):
            pre_gt = mx_banks.tile([P, GROUP_ROWS[g] * P], F32, tag="mx")
            first_layer_pass(g, t, 0, pre_gt)
            first_layer_pass(g, t, 1, pre_gt)
            pre[g, t] = pre_gt

        def first_layer(g):
            edges = GROUP_ROWS[g] * P
            u_g = stage.tile([P, PACK, edges], BF16, tag="u_plain")
            for t in range(PACK):
                if (g, t) not in pre:
                    first_layer_nodes(g, t)
                first_layer_pass(g, t, 2, pre[g, t])
                nc.scalar.activation(
                    out=u_g[:, t, :], in_=pre[g, t][:], func=GELU, bias=b1_col[:, t : t + 1], scale=1.0
                )
            u_plain[g] = u_g

        def regroup_u(g):
            grouped = stage.tile([P, GROUP_ROWS[g] * P * PACK], BF16, align_bytes=256, tag="u_grouped")
            dst, src = side_by_side_views(grouped[:], u_plain[g][:])
            nc.scalar.copy(out=dst, in_=src)
            u_grouped[g] = grouped

        def quantise_u(g):
            codes = stage.tile([P, GROUP_ROWS[g] * P], U32, align_bytes=256, tag="u_codes")
            scales = stage.tile([P, GROUP_ROWS[g] * P], U8, align_bytes=256, tag="u_scales")
            nc.vector.quantize_mx(out=codes[:].bitcast(FP8X4), scales=scales[:], in_=u_grouped[g][:])
            u_q[g] = (codes, scales)

        def second_layer(g):
            codes, scales = u_q[g]
            for r in range(GROUP_ROWS[g]):
                edges = slice(r * P, (r + 1) * P)
                prod = mx_banks.tile([P, D], F32, tag="mx")
                if g == GROUPS - 2 and r == 2:
                    quantise_u(GROUPS - 1)
                nc.tensor.matmul_mx(
                    out=prod[:],
                    lhsT=codes[:, edges].bitcast(FP8X4),
                    lhsT_scale=scales[:, edges],
                    rhs=w_codes[3][:].bitcast(FP8X4),
                    rhs_scale=w_scales[3][:],
                    start=True,
                    stop=True,
                )
                nc.vector.tensor_tensor(out=res[g][:, r, :], in0=prod[:], in1=res[g][:, r, :], op=ADD)
                nc.sync.dma_start(out=out_rows[:, FIRST_ROW[g] + r, :], in_=res[g][:, r, :])

        regroup_weights(0, VECTOR_COLUMNS)
        repeat_scales(0)
        regroup_weights(1, VECTOR_COLUMNS)
        repeat_scales(1)
        spread_hi()
        repeat_scales(2)
        quantise_weights(0)
        repeat_scales(3)
        flip_edges(0)
        b1_wide = keep.tile([P, P], F32)
        nc.vector.tensor_copy(out=b1_wide[:], in_=b1_rows[:])
        b1_flip = mx_banks.tile([P, P], F32, tag="mx")
        nc.tensor.transpose(b1_flip[:], b1_wide[:], ident[:])
        b2_bank = mx_banks.tile([P, D], F32, tag="mx")
        nc.tensor.matmul(out=b2_bank[:], lhsT=ones[:], rhs=b2_row[:], start=True, stop=True)
        quantise_weights(1)
        spread_hj(0)
        regroup_weights(2, VECTOR_COLUMNS)
        flip_edges(1)
        for t in range(PACK):
            first_layer_nodes(0, t)
        quantise_edges(0)
        b1_col = keep.tile([P, PACK], F32)
        nc.vector.tensor_copy(out=b1_col[:], in_=b1_flip[:, 0:PACK])
        quantise_weights(2)
        b2_all = keep.tile([P, D], BF16)

        for r in range(GROUPS + 1):
            if r + 1 < GROUPS and r > 0:
                flip_edges(r + 1)
            if 1 <= r < GROUPS:
                quantise_u(r - 1)
            if r + 1 < GROUPS and r > 0:
                quantise_edges(r + 1)
            if r >= 1 and r < GROUPS:
                residual(r)
            if r < GROUPS:
                first_layer(r)
            if r == 0:
                quantise_edges(1)
                nc.scalar.copy(out=b2_all[:], in_=b2_bank[:])
                spread_hj(1)
                regroup_weights(3, D)
                spread_hj(2)
                quantise_weights(3)
                residual(0)
            if r >= 1 and r + 2 < GROUPS:
                spread_hj(r + 2)
            if r == GROUPS - 1:
                regroup_u(r)
            if r >= 1:
                second_layer(r - 1)
            if r < GROUPS - 1:
                regroup_u(r)
